import numpy as np
import ml_dtypes


def mxq(x, axis, fmt="e4m3"):
    dtype, down = {"e4m3": (ml_dtypes.float8_e4m3fn, 7), "e5m2": (ml_dtypes.float8_e5m2, 14)}[fmt]
    v = np.moveaxis(np.asarray(x, np.float32).astype(ml_dtypes.bfloat16).astype(np.float64), axis, -1)
    blocks = v.reshape(v.shape[:-1] + (-1, 32))
    amax = np.abs(blocks).max(-1, keepdims=True)
    byte = np.maximum(np.where(amax > 0, np.frexp(amax)[1] - 1 + 127, 0) - down, 1)
    scale = np.exp2(byte - 127.0)
    codes = (blocks / scale).astype(np.float32).astype(dtype).astype(np.float64)
    return np.moveaxis((codes * scale).reshape(v.shape), -1, axis)


WIDE = False


def mx_kscale(k):
    if not WIDE:
        return np.ones(k)
    levels = np.array([10, -10, 5, -5, 0])
    if k % 512:
        return np.exp2(np.random.permutation(np.resize(levels, k // 32))).repeat(32)
    a = np.empty((k // 512, 16))
    for p in range(k // 512):
        a[p, :8] = np.random.permutation(np.resize(levels, 8))
        for g in range(8):
            far = levels[np.abs(levels - a[p, g]) >= 10]
            a[p, g + 8] = far[np.random.randint(len(far))]
    return np.exp2(a.ravel()).repeat(32)


BF16 = ml_dtypes.bfloat16


def bf(x):
    return np.asarray(x, np.float32).astype(BF16)


def f64(x):
    return np.asarray(x).astype(np.float64)


B, H, W, C, U, K = 8, 18, 18, 128, 1024, 3
OY, OX = H - K + 1, W - K + 1
T = B * OY * OX
D = K * K * C
P_SCALE = 5.0
Q_SCALE = 0.3
EPS = 1e-6
L2_EPS = 1e-12


def im2col_valid(x, k):
    nb, nh, nw, nc_ = x.shape
    oy, ox = nh - k + 1, nw - k + 1
    patches = np.stack([x[:, i:i + oy, j:j + ox, :] for i in range(k) for j in range(k)], axis=3)
    return patches.reshape(nb, oy * ox, k * k * nc_), oy, ox


def col2im_valid(dp, k, nh, nw):
    nb, oy, ox, _, nc_ = dp.shape
    gx = np.zeros((nb, nh, nw, nc_))
    for i in range(k):
        for j in range(k):
            gx[:, i:i + oy, j:j + ox, :] += dp[:, :, :, i * k + j, :]
    return gx


def image_scale():
    blk = np.sort(mx_kscale(T)[::32])
    pick = (np.arange(B) * (len(blk) - 1)) // (B - 1)
    v = blk[pick]
    sb = np.empty(B)
    sb[0::2] = v[:B // 2]
    sb[1::2] = v[::-1][:B // 2]
    return sb


def cos_parts(x, w, q):
    x, w, q = f64(x), f64(w), f64(q)
    nb = x.shape[0]
    patches, oy, ox = im2col_valid(x, K)
    qq = np.square(q / Q_SCALE)
    x_norm = np.sqrt(np.maximum(np.sum(np.square(patches), axis=2, keepdims=True), L2_EPS)) + qq
    w_norm = np.sqrt(np.maximum(np.sum(np.square(w), axis=1, keepdims=True), L2_EPS)) + qq
    sim = (patches / x_norm) @ (w / w_norm)
    return (1.0 / x_norm).reshape(nb, oy, ox), (1.0 / w_norm).reshape(-1), sim.reshape(nb, oy, ox, w.shape[2])


def setup_inputs():
    sb = image_scale()[:, None, None, None]
    u = mx_kscale(U)
    g = np.random.uniform(0.5, 1.5, (1, 1, U)) * np.sign(np.random.standard_normal((1, 1, U)))
    x0 = bf(np.abs(np.random.standard_normal((B, H, W, C))) * 0.25)
    w0 = bf((np.random.standard_normal((1, D, U)) + g) * 2.0 / np.sqrt(D))
    p = bf(0.7 * P_SCALE * (1.0 + 0.1 * np.random.standard_normal(U)))
    q = bf(0.2 * (1.0 + 0.1 * np.random.standard_normal(1)))
    go = bf(np.random.standard_normal((B, OY, OX, U)) * np.exp2(np.random.randint(-6, 1, (B, OY, OX, 1))) * 32.0 / sb * u)
    rx, rw, sim = cos_parts(x0, w0, q)
    return {"x": bf(f64(x0) * sb), "w": bf(f64(w0) / u[None, None, :]), "p": p, "q": q,
            "x_rnorm": np.asarray(rx, np.float32), "w_rnorm": np.asarray(rw, np.float32),
            "sim": np.asarray(sim, np.float32), "grad_out": go}


def reference(x, w, p, q, x_rnorm, w_rnorm, sim, grad_out):
    x, w, p, q = f64(x), f64(w), f64(p), f64(q)
    w2 = w[0]
    rx = f64(x_rnorm).reshape(T, 1)
    rw = f64(w_rnorm).reshape(1, U)
    patches = im2col_valid(x, K)[0].reshape(T, D)
    xn = patches * rx
    wn = w2 * rw
    pp = np.square(p / P_SCALE)
    sm = f64(sim).reshape(T, U)
    dsim = f64(grad_out).reshape(T, U) * pp * np.power(np.abs(sm) + EPS, pp - 1.0)
    dxn = mxq(dsim, 1, "e5m2") @ mxq(wn, 1, "e4m3").T
    dwn = mxq(xn, 0, "e4m3").T @ mxq(dsim, 0, "e5m2")
    qq = np.square(q / Q_SCALE)
    sx = np.sum(np.square(patches), axis=1, keepdims=True)
    cx = np.sum(dxn * patches, axis=1, keepdims=True)
    dpat = rx * (dxn - patches * (cx / sx) * (1.0 - qq * rx))
    gx = col2im_valid(dpat.reshape(B, OY, OX, K * K, C), K, H, W)
    sw = np.sum(np.square(w2), axis=0, keepdims=True)
    cw = np.sum(dwn * w2, axis=0, keepdims=True)
    gw = rw * (dwn - w2 * (cw / sw) * (1.0 - qq * rw))
    return gx, gw[None]

@@ -1,0 +1,626 @@
+from contextlib import ExitStack
+
+import concourse.mybir as mybir
+from concourse.masks import make_identity
+
+F32 = mybir.dt.float32
+BF16 = mybir.dt.bfloat16
+I32 = mybir.dt.int32
+U32 = mybir.dt.uint32
+U8 = mybir.dt.uint8
+E4 = mybir.dt.float8_e4m3fn_x4
+E5 = mybir.dt.float8_e5m2_x4
+ALU = mybir.AluOpType
+ACT = mybir.ActivationFunctionType
+AX = mybir.AxisListType
+
+P = 128
+NB = 8
+NH = 18
+NY = 16
+U = 1024
+D = 1152
+T = 2048
+FLOPS = 2 * 2 * T * D * U
+
+DX_WINDOWS = ((0, 0), (384, 0), (640, 128))
+DW_WINDOWS = ((0, 0, 512, 0), (512, 0, 512, 512), (640, 384, 128, 1024))
+
+O_DTC = 0
+O_DTS = 16384
+O_XC = 20480
+O_HA = 34304
+O_WT = 61952
+O_WNC = 80384
+O_WNS = 89600
+O_SIM = (91904, 108288)
+O_LG = (124672, 141056)
+O_GO = (157440, 165632)
+O_UF = (173824, 177920)
+O_PL = (182016, 190208)
+O_UC = (198400, 202496)
+O_US = (206592, 207616)
+O_TF = 208640
+O_JV = 216832
+O_JS = 218368
+O_XNC = 157440
+O_XNS = 175872
+O_WSB = 157440
+O_WN = 34304
+O_JW = 194304
+O_F1 = 91904
+O_R0 = 128768
+O_R2 = 137984
+O_OT = (147200, 149248, 151296, 153344)
+O_JC = 155392
+O_JW2 = 219392
+O_XI = (108288, 117504)
+O_XS = (126720, 135936)
+
+U_ON_SCALAR = ((3, 0), (3, 1))
+N_ON_SCALAR = (0, 1)
+
+
+def tile_cossim2d_v_kernel(tc, x, w, p, q, x_rnorm, w_rnorm, sim, grad_out, out_0, out_1):
+    nc = tc.nc
+
+    with ExitStack() as ctx:
+        keep = ctx.enter_context(tc.tile_pool(name="keep", bufs=1))
+        big = ctx.enter_context(tc.tile_pool(name="big", bufs=1))
+        psum = ctx.enter_context(tc.psum_pool(name="psum", bufs=2))
+        ctx.enter_context(tc.manual_schedule())
+
+        def bank(kind):
+            ps = psum.tile([P, 512], F32, name="ps_" + kind, tag=kind, bufs=4 if kind == "mm" else 2)
+            return ps
+
+        ident = keep.tile([P, P], F32, name="ident")
+        make_identity(nc, ident[:])
+        eps_c = keep.tile([P, 1], F32, name="eps_c")
+        nc.vector.memset(eps_c[:], 1e-6)
+        p_c = keep.tile([P, 8], BF16, name="p_c")
+        rw_c = keep.tile([P, 8], F32, name="rw_c")
+        q_c = keep.tile([P, 1], BF16, name="q_c")
+        rx_c = keep.tile([P, NY], F32, name="rx_c")
+        rx_t = keep.tile([P, 14, 2], F32, name="rx_t")
+        nc.sync.dma_start(out=p_c[:].rearrange("p (g t) -> p g t", g=2), in_=p.rearrange("(g p t) -> p g t", g=2, t=4))
+        nc.sync.dma_start(out=rw_c[:].rearrange("p (g t) -> p g t", g=2), in_=w_rnorm.rearrange("(g p t) -> p g t", g=2, t=4))
+        nc.sync.dma_start(out=q_c[:], in_=q.partition_broadcast(P))
+
+        wn_codes = big.tile([P, 2, D], U32, name="wn_codes", offset=O_WNC, align_bytes=64)
+        wn_scales = big.tile([P, 2, D], U8, name="wn_scales", offset=O_WNS, align_bytes=64)
+        xn_codes = big.tile([P, 4, D], U32, name="xn_codes", offset=O_XNC, align_bytes=64)
+        xn_scales = big.tile([P, 4, D], U8, name="xn_scales", offset=O_XNS, align_bytes=64)
+        dt_codes = big.tile([P, 4, U], U32, name="dt_codes", offset=O_DTC, align_bytes=64)
+        dt_scales = big.tile([P, 4, U], U8, name="dt_scales", offset=O_DTS, align_bytes=64)
+        xc = big.tile([P, NH, 384], BF16, name="xc", offset=O_XC, align_bytes=64)
+        ha = big.tile([P, NH, 384], F32, name="ha", offset=O_HA, align_bytes=64)
+        wt = big.tile([P, 2, D, 4], BF16, name="wt", offset=O_WT, align_bytes=64)
+        junk_v = big.tile([P, 384], F32, name="junk_v", offset=O_JV, align_bytes=64)
+        junk_s = big.tile([P, 384], BF16, name="junk_s", offset=O_JS, align_bytes=64)
+        sw_c = keep.tile([P, 8], F32, name="sw_c")
+        rs_c = keep.tile([P, NH], F32, name="rs_c")
+        cx_p = keep.tile([P, NY, 3], F32, name="cx_p")
+        cw_p = keep.tile([P, 8, 3], F32, name="cw_p")
+        e_c = keep.tile([P, 8], F32, name="e_c")
+        em1_c = keep.tile([P, 8], F32, name="em1_c")
+        lne_c = keep.tile([P, 8], F32, name="lne_c")
+        qq_c = keep.tile([P, 1], F32, name="qq_c")
+
+        sims = {}
+        logs = {}
+        gos = {}
+        plains = {}
+        ucodes = {}
+        tfs = {}
+        xts = {}
+
+        def chunk_off(yy):
+            return (yy % 2) * 256 + (yy // 2) * 128
+
+        w_sb = big.tile([P, 9, U], BF16, name="w_sb", offset=O_WSB, align_bytes=64)
+
+        def ld_w():
+            for k0 in range(0, 9, 3):
+                nc.sync.dma_start(out=w_sb[:, k0 : k0 + 3, :], in_=w[0, 128 * k0 : 128 * (k0 + 3), :].rearrange("(k p) u -> p k u", p=P))
+
+        def ld_sim(c):
+            s_sb = big.tile([P, 4, U], F32, name="s_sb%d" % c, offset=O_SIM[c % 2], align_bytes=64)
+            sims[c] = s_sb
+            for b in range(NB):
+                nc.sync.dma_start(out=s_sb[16 * b : 16 * b + 16, :, :], in_=sim[b, 4 * c : 4 * c + 4].rearrange("y z u -> z y u"))
+
+        def ld_go(c):
+            go = big.tile([P, 4, U], BF16, name="go%d" % c, offset=O_GO[c % 2], align_bytes=64)
+            gos[c] = go
+            for b in range(NB):
+                nc.sync.dma_start(out=go[16 * b : 16 * b + 16, :, :], in_=grad_out[b, 4 * c : 4 * c + 4].rearrange("y z u -> z y u"))
+
+        def ld_xc():
+            xc4 = xc[:].rearrange("p h (j c) -> p h j c", j=3)
+            for j in range(3):
+                for b in range(NB):
+                    nc.sync.dma_start(out=xc4[16 * b : 16 * b + 16, :, j, :], in_=x[b, :, j : j + 16, :].rearrange("h v c -> v h c"))
+
+        def ld_rx():
+            with nc.allow_non_contiguous_dma(reason="2048 single floats, once"):
+                for b in range(NB):
+                    nc.sync.dma_start(out=rx_c[16 * b : 16 * b + 16, :], in_=x_rnorm[b].rearrange("y z -> z y"))
+            for yh in range(2):
+                for b in range(NB):
+                    nc.sync.dma_start(
+                        out=rx_t[64 * yh + 8 * b : 64 * yh + 8 * b + 8, :, :],
+                        in_=x_rnorm[b, 2 * yh : 2 * yh + 14, :].rearrange("r (zw e) -> zw r e", e=2),
+                    )
+
+        def ld_xw():
+            xw = big.tile([P, 16, 512], BF16, name="xw", offset=O_SIM[0], align_bytes=64)
+            xts[0] = xw
+            xw4 = xw[:].rearrange("p r (a m) -> p r a m", a=2)
+            for yh in range(2):
+                for a in range(2):
+                    for b in range(NB):
+                        p0 = 64 * yh + 8 * b
+                        nc.sync.dma_start(
+                            out=xw4[p0 : p0 + 8, :, a, :],
+                            in_=x[b, 2 * yh : 2 * yh + 16, 2 * a : 2 * a + 16, :].rearrange("r (zw e) c -> zw r (e c)", e=2),
+                        )
+
+        def small_consts():
+            nc.scalar.activation(out=e_c[:], in_=p_c[:], func=ACT.Square, scale=0.2)
+            nc.vector.tensor_scalar_add(out=em1_c[:], in0=e_c[:], scalar1=-1.0)
+            nc.scalar.activation(out=lne_c[:], in_=e_c[:], func=ACT.Ln)
+            nc.scalar.activation(out=qq_c[:], in_=q_c[:], func=ACT.Square, scale=1.0 / 0.3)
+
+        def w_turn():
+            ww = w_sb[:].rearrange("p k u -> p (k u)").bitcast(F32)
+            wtw = wt[:].rearrange("p g d t -> p (g d t)").bitcast(F32).rearrange("p (g d h) -> p g d h", g=2, h=2)
+            for g in range(2):
+                for k0 in range(0, 9, 2):
+                    nk = min(2, 9 - k0)
+                    ps = bank("ts")
+                    for h in range(2):
+                        for kk in range(nk):
+                            c0 = (k0 + kk) * 512 + 256 * g
+                            nc.tensor.transpose(ps[:, h * 256 + kk * 128 : h * 256 + (kk + 1) * 128], ww[:, c0 + h : c0 + 256 : 2], ident[:])
+                    nc.scalar.copy(
+                        out=wtw[:, g, k0 * 128 : (k0 + nk) * 128, :],
+                        in_=ps[:].rearrange("p (h c) -> p c h", h=2)[:, 0 : nk * 128, :],
+                    )
+
+        wn = big.tile([P, 2, D, 4], BF16, name="wn", offset=O_WN, align_bytes=64)
+
+        def w_scale():
+            for g, eng in ((0, nc.gpsimd), (1, nc.vector)):
+                eng.tensor_tensor(
+                    out=wn[:, g], in0=wt[:, g], in1=rw_c[:, 4 * g : 4 * g + 4].unsqueeze(1).to_broadcast([P, D, 4]), op=ALU.mult
+                )
+
+        def w_quant():
+            wnf = wn[:].rearrange("p g d t -> p g (d t)")
+            for g in range(2):
+                for d0, d1 in ((0, 1024), (1024, D)):
+                    nc.vector.quantize_mx(
+                        out=wn_codes[:, g, d0:d1].bitcast(E4), scales=wn_scales[:, g, d0:d1], in_=wnf[:, g, 4 * d0 : 4 * d1]
+                    )
+
+        junk_w = big.tile([P, D], BF16, name="junk_w", offset=O_JW2, align_bytes=64)
+
+        def w_squares(k):
+            nc.scalar.activation(out=junk_w[:], in_=wt[:, k // 4, :, k % 4], func=ACT.Square, accum_out=sw_c[:, k : k + 1])
+
+        def x_squares(h):
+            nc.scalar.activation(out=junk_s[:], in_=xc[:, h, :], func=ACT.Square, accum_out=rs_c[:, h : h + 1])
+
+        def new_log(c):
+            logs[c] = big.tile([P, 8, 512], F32, name="lg%d" % c, offset=O_LG[c % 2], align_bytes=64)
+
+        def v_abs(c, yy):
+            v = sims[c][:, yy, :].bitcast(I32)
+            nc.vector.tensor_scalar(out=v, in0=v, scalar1=0x7FFFFFFF, scalar2=None, op0=ALU.bitwise_and)
+
+        def a_step(c, yy):
+            s_sb = sims[c]
+            lg = logs[c]
+            off = chunk_off(yy)
+            for g in range(2):
+                ps = bank("ts")
+                for t in range(4):
+                    nc.tensor.transpose(ps[:, t * 128 : (t + 1) * 128], s_sb[:, yy, 512 * g + t : 512 * (g + 1) : 4], ident[:])
+                nc.scalar.activation(
+                    out=lg[:, 4 * g : 4 * g + 4, off : off + 128],
+                    in_=ps[:].rearrange("p (t c) -> p t c", t=4),
+                    func=ACT.Ln,
+                    bias=eps_c[:, 0:1],
+                )
+
+        def e_step(c, k):
+            lg = logs[c]
+            nc.scalar.activation(out=lg[:, k, :], in_=lg[:, k, :], func=ACT.Exp, bias=lne_c[:, k : k + 1], scale=em1_c[:, k : k + 1])
+
+        def new_plain(c):
+            plains[c] = big.tile([P, 8, 512], BF16, name="pl%d" % c, offset=O_PL[c % 2], align_bytes=64)
+
+        gts = {}
+
+        def m_pe(c, yy):
+            gw = gos[c][:].rearrange("p y u -> p (y u)").bitcast(F32)
+            ps = bank("tv")
+            gts[(c, yy)] = ps
+            for gh in range(4):
+                c0 = yy * 512 + 256 * (gh // 2)
+                nc.tensor.transpose(ps[:, gh * 128 : (gh + 1) * 128], gw[:, c0 + gh % 2 : c0 + 256 : 2], ident[:])
+
+        def m_v(c, yy):
+            pl = plains[c]
+            lg = logs[c]
+            off = chunk_off(yy)
+            ps = gts[(c, yy)]
+            nc.vector.tensor_tensor(
+                out=pl[:, :, off : off + 128].rearrange("p (k e) c -> p k e c", e=2),
+                in0=lg[:, :, off : off + 128].rearrange("p (k e) c -> p k e c", e=2),
+                in1=ps[:].bitcast(BF16).rearrange("p (k c e) -> p k e c", k=4, e=2),
+                op=ALU.mult,
+            )
+
+        def u_copy(c, g):
+            if g == 0:
+                uc = big.tile([P, 2, 512], U32, name="uc%d" % c, offset=O_UC[c % 2], align_bytes=64)
+                us = big.tile([P, 2, 512], U8, name="us%d" % c, offset=O_US[c % 2], align_bytes=64)
+                ucodes[c] = [uc, us, None, None]
+            uf = big.tile([P, 512, 4], BF16, name="uf%d_%d" % (c, g), offset=O_UF[g], align_bytes=64)
+            ucodes[c][2 + g] = uf
+            src = plains[c][:, 4 * g : 4 * g + 4, :].rearrange("p t c -> p c t")
+            if (c, g) in U_ON_SCALAR:
+                nc.scalar.copy(out=uf[:], in_=src)
+            else:
+                nc.vector.tensor_copy(out=uf[:], in_=src)
+
+        def u_quant(c, g):
+            uc, us = ucodes[c][0], ucodes[c][1]
+            uf = ucodes[c][2 + g]
+            nc.vector.quantize_mx(out=uc[:, g, :].bitcast(E5), scales=us[:, g, :], in_=uf[:].rearrange("p c t -> p (c t)"))
+
+        def t_step(c, kp):
+            if kp == 0:
+                tfs[c] = big.tile([P, U, 4], BF16, name="tf%d" % c, offset=O_TF, align_bytes=64)
+            plw = plains[c][:].rearrange("p k c -> p (k c)").bitcast(F32)
+            tfw = tfs[c][:].rearrange("p u t -> p (u t)").bitcast(F32).rearrange("p (u l) -> p u l", l=2)
+            ps = bank("ts")
+            for l in range(2):
+                for kk in range(2):
+                    c0 = (2 * kp + kk) * 256 + l * 128
+                    nc.tensor.transpose(ps[:, l * 256 + kk * 128 : l * 256 + (kk + 1) * 128], plw[:, c0 : c0 + 128], ident[:])
+            nc.scalar.copy(out=tfw[:, kp * 256 : (kp + 1) * 256, :], in_=ps[:].rearrange("p (l c) -> p c l", l=2))
+
+        def t_quant(c):
+            nc.vector.quantize_mx(out=dt_codes[:, c, :].bitcast(E5), scales=dt_scales[:, c, :], in_=tfs[c][:].rearrange("p u t -> p (u t)"))
+
+        touched = set()
+
+        def x_step(c, yy):
+            uc, us = ucodes[c][0], ucodes[c][1]
+            y = 4 * c + yy
+            co = chunk_off(yy)
+            for i in (2, 0, 1):
+                ws, uo = DX_WINDOWS[i]
+                ps = bank("mm")
+                for g in range(2):
+                    nc.tensor.matmul_mx(
+                        out=ps[:],
+                        lhsT=uc[:, g, co : co + 128].bitcast(E5),
+                        lhsT_scale=us[:, g, co : co + 128],
+                        rhs=wn_codes[:, g, ws : ws + 512].bitcast(E4),
+                        rhs_scale=wn_scales[:, g, ws : ws + 512],
+                        start=(g == 0),
+                        stop=(g == 1),
+                    )
+                h = y + i
+                if h not in touched:
+                    touched.add(h)
+                    nc.scalar.activation(out=ha[:, h, :], in_=ps[:, uo : uo + 384], func=ACT.Copy, scale=rx_c[:, y : y + 1])
+                else:
+                    nc.vector.scalar_tensor_tensor(
+                        out=ha[:, h, :], in0=ps[:, uo : uo + 384], scalar=rx_c[:, y : y + 1], in1=ha[:, h, :], op0=ALU.mult, op1=ALU.add
+                    )
+                nc.vector.scalar_tensor_tensor(
+                    out=junk_v[:], in0=ps[:, uo : uo + 384], scalar=1.0, in1=xc[:, h, :],
+                    op0=ALU.mult, op1=ALU.mult, accum_out=cx_p[:, y, i : i + 1],
+                )
+
+        def n_scale(c):
+            xw = xts[0]
+            xs = big.tile([P, 4, 3, 384], BF16, name="xs%d" % c, offset=O_XS[c % 2], align_bytes=64)
+            xts[("s", c)] = xs
+            for l in range(2):
+                for e in range(2):
+                    r0 = 4 * c + l
+                    nc.vector.tensor_scalar_mul(
+                        out=xs[:, 2 * l + e, :, :], in0=xw[:, r0 : r0 + 3, e * 128 : e * 128 + 384], scalar1=rx_t[:, r0, e : e + 1]
+                    )
+
+        def n_copy(c, i):
+            if i == 0:
+                xts[("i", c)] = big.tile([P, D, 4], BF16, name="xi%d" % c, offset=O_XI[c % 2], align_bytes=64)
+            xi = xts[("i", c)]
+            src = xts[("s", c)][:, :, i, :].rearrange("p t m -> p m t")
+            if c in N_ON_SCALAR:
+                nc.scalar.copy(out=xi[:, 384 * i : 384 * (i + 1), :], in_=src)
+            else:
+                nc.vector.tensor_copy(out=xi[:, 384 * i : 384 * (i + 1), :], in_=src)
+
+        def n_quant(c):
+            xif = xts[("i", c)][:].rearrange("p d t -> p (d t)")
+            for d0, d1 in ((0, 1024), (1024, D)):
+                nc.vector.quantize_mx(out=xn_codes[:, c, d0:d1].bitcast(E4), scales=xn_scales[:, c, d0:d1], in_=xif[:, 4 * d0 : 4 * d1])
+
+        later = []
+
+        def fill(n):
+            for r in range(min(n, len(later))):
+                f, a = later.pop(0)
+                f(*a)
+
+        ld_w()
+        ld_sim(0)
+        ld_sim(1)
+        small_consts()
+        w_turn()
+        ld_go(0)
+        ld_rx()
+        ld_xc()
+        ld_go(1)
+        new_log(0)
+        for yy in range(4):
+            v_abs(0, yy)
+            a_step(0, yy)
+        w_scale()
+        for k in range(8):
+            e_step(0, k)
+        m_pe(0, 0)
+        m_pe(0, 1)
+        for yy in range(4):
+            v_abs(1, yy)
+        new_log(1)
+        a_step(1, 0)
+        ld_sim(2)
+        w_quant()
+        new_plain(0)
+        m_v(0, 0)
+        m_pe(0, 2)
+        m_v(0, 1)
+        m_pe(0, 3)
+        for yy in range(1, 4):
+            a_step(1, yy)
+        m_v(0, 2)
+        m_v(0, 3)
+        ld_sim(3)
+        ld_go(2)
+        for g in range(2):
+            u_copy(0, g)
+        for kp in range(4):
+            t_step(0, kp)
+        for g in range(2):
+            u_quant(0, g)
+        t_quant(0)
+        m_pe(1, 0)
+        m_pe(1, 1)
+        new_log(2)
+        for yy in range(4):
+            if yy < 2:
+                for k in range(4 * yy, 4 * yy + 4):
+                    e_step(1, k)
+                v_abs(2, 2 * yy)
+                v_abs(2, 2 * yy + 1)
+            x_step(0, yy)
+            if yy >= 2:
+                a_step(2, 2 * yy - 4)
+                a_step(2, 2 * yy - 3)
+        new_plain(1)
+        m_v(1, 0)
+        m_pe(1, 2)
+        m_v(1, 1)
+        m_pe(1, 3)
+        m_v(1, 2)
+        m_v(1, 3)
+        ld_go(3)
+        ld_xw()
+        for k in range(8):
+            later.append((w_squares, (k,)))
+        for h in range(NH):
+            later.append((x_squares, (h,)))
+        for yy in range(4):
+            v_abs(3, yy)
+        for kp in range(4):
+            t_step(1, kp)
+        new_log(3)
+        for yy in range(4):
+            a_step(3, yy)
+        for g in range(2):
+            u_copy(1, g)
+        for g in range(2):
+            u_quant(1, g)
+        t_quant(1)
+        m_pe(2, 0)
+        m_pe(2, 1)
+        for yy in range(4):
+            x_step(1, yy)
+            e_step(2, 2 * yy)
+            e_step(2, 2 * yy + 1)
+        new_plain(2)
+        m_v(2, 0)
+        m_pe(2, 2)
+        m_v(2, 1)
+        m_pe(2, 3)
+        m_v(2, 2)
+        m_v(2, 3)
+        for k in range(8):
+            e_step(3, k)
+        for g in range(2):
+            u_copy(2, g)
+        for kp in range(4):
+            t_step(2, kp)
+        fill(6)
+        m_pe(3, 0)
+        m_pe(3, 1)
+        for g in range(2):
+            u_quant(2, g)
+        t_quant(2)
+        new_plain(3)
+        m_v(3, 0)
+        m_pe(3, 2)
+        m_v(3, 1)
+        m_pe(3, 3)
+        m_v(3, 2)
+        m_v(3, 3)
+        for g in range(2):
+            u_copy(3, g)
+        for kp in range(4):
+            t_step(3, kp)
+        n_scale(0)
+        n_scale(1)
+        for c in range(2):
+            for i in range(3):
+                later.insert(3 * c + i, (n_copy, (c, i)))
+        for yy in range(4):
+            x_step(2, yy)
+            fill(1)
+            if yy == 1:
+                for g in range(2):
+                    u_quant(3, g)
+                t_quant(3)
+        fill(2)
+        n_quant(0)
+        for yy in range(4):
+            x_step(3, yy)
+            fill(1 if yy == 0 else 3)
+            if yy == 0:
+                n_scale(2)
+                for i in range(3):
+                    n_copy(2, i)
+            if yy == 1:
+                n_quant(1)
+                n_quant(2)
+            if yy == 2:
+                n_scale(3)
+                for i in range(3):
+                    n_copy(3, i)
+        n_quant(3)
+        fill(len(later))
+
+        sx = keep.tile([P, NY], F32, name="sx")
+        fx = keep.tile([P, NY], F32, name="fx")
+        cx = keep.tile([P, NY], F32, name="cx")
+        ns = keep.tile([P, NH], F32, name="ns")
+        fw = keep.tile([P, 8], F32, name="fw")
+        rsw = keep.tile([P, 8], F32, name="rsw")
+        cw = keep.tile([P, 8], F32, name="cw")
+        f1 = big.tile([P, 8, D], F32, name="f1", offset=O_F1, align_bytes=64)
+        junk_c = big.tile([P, 512], F32, name="junk_c", offset=O_JC, align_bytes=64)
+        r0 = big.tile([P, NH, 128], F32, name="r0", offset=O_R0, align_bytes=64)
+        r2 = big.tile([P, NH, 128], F32, name="r2", offset=O_R2, align_bytes=64)
+        ha4 = ha[:].rearrange("p h (j c) -> p h j c", j=3)
+        flat1 = out_1.rearrange("o d u -> (o d u)")
+        park0 = flat1[0 : P * NH * 128].rearrange("(p h c) -> p h c", p=P, c=128)
+        park2 = flat1[P * NH * 128 : 2 * P * NH * 128].rearrange("(p h c) -> p h c", p=P, c=128)
+
+        def dw_mm(k):
+            res = []
+            for wi in range(3):
+                ws = DW_WINDOWS[wi][0]
+                ps = bank("mm")
+                res.append(ps)
+                for c in range(4):
+                    nc.tensor.matmul_mx(
+                        out=ps[:],
+                        lhsT=dt_codes[:, c, k * 128 : (k + 1) * 128].bitcast(E5),
+                        lhsT_scale=dt_scales[:, c, k * 128 : (k + 1) * 128],
+                        rhs=xn_codes[:, c, ws : ws + 512].bitcast(E4),
+                        rhs_scale=xn_scales[:, c, ws : ws + 512],
+                        start=(c == 0),
+                        stop=(c == 3),
+                    )
+                ws, uo, n, d0 = DW_WINDOWS[wi]
+                nc.vector.scalar_tensor_tensor(
+                    out=junk_c[:, 0:n], in0=ps[:, uo : uo + n], scalar=1.0, in1=wt[:, k // 4, d0 : d0 + n, k % 4],
+                    op0=ALU.mult, op1=ALU.mult, accum_out=cw_p[:, k, wi : wi + 1],
+                )
+                nc.scalar.activation(out=f1[:, k, d0 : d0 + n], in_=ps[:, uo : uo + n], func=ACT.Copy, scale=rw_c[:, k : k + 1])
+
+        def x_factors():
+            nc.vector.tensor_tensor(out=sx[:], in0=rs_c[:, 0:16], in1=rs_c[:, 1:17], op=ALU.add)
+            nc.vector.tensor_tensor(out=sx[:], in0=sx[:], in1=rs_c[:, 2:18], op=ALU.add)
+            nc.vector.reciprocal(out=sx[:], in_=sx[:])
+            nc.vector.tensor_scalar(out=fx[:], in0=rx_c[:], scalar1=qq_c[:, 0:1], scalar2=-1.0, op0=ALU.mult, op1=ALU.add)
+            nc.vector.tensor_tensor(out=fx[:], in0=fx[:], in1=rx_c[:], op=ALU.mult)
+            nc.vector.tensor_tensor(out=fx[:], in0=fx[:], in1=sx[:], op=ALU.mult)
+            nc.vector.tensor_reduce(out=cx[:], in_=cx_p[:], axis=AX.X, op=ALU.add)
+            nc.vector.tensor_tensor(out=cx[:], in0=cx[:], in1=fx[:], op=ALU.mult)
+            nc.vector.memset(ns[:], 0.0)
+            for i in range(3):
+                nc.vector.tensor_tensor(out=ns[:, i : i + 16], in0=ns[:, i : i + 16], in1=cx[:], op=ALU.add)
+
+        def w_factors():
+            nc.vector.reciprocal(out=rsw[:], in_=sw_c[:])
+            nc.vector.tensor_scalar(out=fw[:], in0=rw_c[:], scalar1=qq_c[:, 0:1], scalar2=-1.0, op0=ALU.mult, op1=ALU.add)
+            nc.vector.tensor_tensor(out=fw[:], in0=fw[:], in1=rw_c[:], op=ALU.mult)
+            nc.vector.tensor_tensor(out=fw[:], in0=fw[:], in1=rsw[:], op=ALU.mult)
+
+        def x_norm_term(h):
+            nc.vector.scalar_tensor_tensor(
+                out=ha[:, h, :], in0=xc[:, h, :], scalar=ns[:, h : h + 1], in1=ha[:, h, :], op0=ALU.mult, op1=ALU.add
+            )
+
+        def park():
+            nc.sync.dma_start(out=park0, in_=ha4[:, :, 0, :])
+            nc.sync.dma_start(out=park2, in_=ha4[:, :, 2, :])
+            nc.sync.dma_start(out=out_0[:, :, 0, :], in_=ha4[0:P:16, :, 0, :])
+            nc.sync.dma_start(out=out_0[:, :, 17, :], in_=ha4[15:P:16, :, 2, :])
+            for b in range(NB):
+                nc.sync.dma_start(out=r0[16 * b : 16 * b + 15], in_=park0[16 * b + 1 : 16 * b + 16])
+                nc.sync.dma_start(out=r2[16 * b + 1 : 16 * b + 16], in_=park2[16 * b : 16 * b + 15])
+
+        def x_finish():
+            nc.gpsimd.tensor_tensor(out=r0[:], in0=r0[:], in1=ha4[:, :, 1, :], op=ALU.add)
+            nc.gpsimd.tensor_tensor(out=r0[:], in0=r0[:], in1=r2[:], op=ALU.add)
+            for b in range(NB):
+                nc.gpsimd.dma_start(out=out_0[b, :, 1:17, :].rearrange("h v c -> v h c"), in_=r0[16 * b : 16 * b + 16])
+
+        def w_coef(k):
+            nc.vector.tensor_reduce(out=cw[:, k : k + 1], in_=cw_p[:, k, :], axis=AX.X, op=ALU.add)
+            nc.vector.tensor_tensor(out=cw[:, k : k + 1], in0=cw[:, k : k + 1], in1=fw[:, k : k + 1], op=ALU.mult)
+
+        def w_final(k):
+            nc.vector.scalar_tensor_tensor(
+                out=f1[:, k, :], in0=wt[:, k // 4, :, k % 4], scalar=cw[:, k : k + 1], in1=f1[:, k, :], op0=ALU.mult, op1=ALU.add
+            )
+
+        def w_store(g, kd, n):
+            ps = bank("ts")
+            for t in range(4):
+                nc.tensor.transpose(ps[:, t * 128 : (t + 1) * 128], f1[:, 4 * g + t, kd * 128 : (kd + 1) * 128], ident[:])
+            ot = big.tile([P, 512], F32, name="ot%d_%d" % (g, kd), offset=O_OT[n % 4], align_bytes=64)
+            nc.scalar.copy(out=ot[:].rearrange("p (u t) -> p u t", t=4), in_=ps[:].rearrange("p (t u) -> p u t", t=4))
+            nc.sync.dma_start(out=out_1[0, kd * 128 : (kd + 1) * 128, 512 * g : 512 * (g + 1)], in_=ot[:])
+
+        nc.gpsimd.memset(r0[:], 0.0)
+        nc.gpsimd.memset(r2[:], 0.0)
+        w_factors()
+        x_factors()
+        for k in range(4):
+            for h in range(9 * k, min(9 * k + 9, NH)):
+                x_norm_term(h)
+            if k == 2:
+                park()
+                x_finish()
+            dw_mm(k)
+            w_coef(k)
+            w_final(k)
+        for k in range(4, 8):
+            dw_mm(k)
+            w_coef(k)
+            w_final(k)
+            for n in range(3 * (k - 4), min(3 * (k - 4) + 3, 9)):
+                w_store(0, 8 - n, n)
+        for n in range(9):
+            w_store(1, 8 - n, n + 1)

@@ -76,6 +76,12 @@ def tile_cossim2d_v_kernel(tc, x, w, p, q, x_rnorm, w_rnorm, sim, grad_out, out_
 
         ident = keep.tile([P, P], F32, name="ident")
         make_identity(nc, ident[:])
+        perm = keep.tile([P, P], F32, name="perm")
+        nc.gpsimd.memset(perm[:], 0.0)
+        nc.gpsimd.affine_select(
+            out=perm[:], in_=perm[:], compare_op=ALU.not_equal, fill=1.0, base=0,
+            pattern=[[-16, 2], [-32, 4], [-1, 16]], channel_multiplier=1,
+        )
         eps_c = keep.tile([P, 1], F32, name="eps_c")
         nc.vector.memset(eps_c[:], 1e-6)
         p_c = keep.tile([P, 8], BF16, name="p_c")
@@ -127,30 +133,34 @@ def tile_cossim2d_v_kernel(tc, x, w, p, q, x_rnorm, w_rnorm, sim, grad_out, out_
         def ld_sim(c):
             s_sb = big.tile([P, 4, U], F32, name="s_sb%d" % c, offset=O_SIM[c % 2], align_bytes=64)
             sims[c] = s_sb
-            for b in range(NB):
-                nc.sync.dma_start(out=s_sb[16 * b : 16 * b + 16, :, :], in_=sim[b, 4 * c : 4 * c + 4].rearrange("y z u -> z y u"))
+            hh, bq = c // 2, c % 2
+            for bb in range(4):
+                nc.sync.dma_start(out=s_sb[:, bb, :], in_=sim[4 * bq + bb, 8 * hh : 8 * hh + 8].rearrange("y z u -> (y z) u"))
 
         def ld_go(c):
             go = big.tile([P, 4, U], BF16, name="go%d" % c, offset=O_GO[c % 2], align_bytes=64)
             gos[c] = go
-            for b in range(NB):
-                nc.sync.dma_start(out=go[16 * b : 16 * b + 16, :, :], in_=grad_out[b, 4 * c : 4 * c + 4].rearrange("y z u -> z y u"))
+            hh, bq = c // 2, c % 2
+            for b2 in range(2):
+                nc.sync.dma_start(
+                    out=go[:, 2 * b2 : 2 * b2 + 2, :],
+                    in_=grad_out[4 * bq + 2 * b2 : 4 * bq + 2 * b2 + 2, 8 * hh : 8 * hh + 8].rearrange("b y z u -> (y z) b u"),
+                )
 
         def ld_xc():
             xc4 = xc[:].rearrange("p h (j c) -> p h j c", j=3)
             for j in range(3):
                 for b in range(NB):
-                    nc.sync.dma_start(out=xc4[16 * b : 16 * b + 16, :, j, :], in_=x[b, :, j : j + 16, :].rearrange("h v c -> v h c"))
+                    nc.scalar.dma_start(out=xc4[b:P:8, :, j, :], in_=x[b, :, j : j + 16, :].rearrange("h v c -> v h c"))
 
         def ld_rx():
             with nc.allow_non_contiguous_dma(reason="2048 single floats, once"):
                 for b in range(NB):
-                    nc.sync.dma_start(out=rx_c[16 * b : 16 * b + 16, :], in_=x_rnorm[b].rearrange("y z -> z y"))
+                    nc.scalar.dma_start(out=rx_c[b:P:8, :], in_=x_rnorm[b].rearrange("y z -> z y"))
             for yh in range(2):
-                for b in range(NB):
-                    nc.sync.dma_start(
-                        out=rx_t[64 * yh + 8 * b : 64 * yh + 8 * b + 8, :, :],
-                        in_=x_rnorm[b, 2 * yh : 2 * yh + 14, :].rearrange("r (zw e) -> zw r e", e=2),
+                for zw in range(8):
+                    nc.scalar.dma_start(
+                        out=rx_t[64 * yh + zw : 64 * yh + 64 : 8, :, :], in_=x_rnorm[:, 2 * yh : 2 * yh + 14, 2 * zw : 2 * zw + 2]
                     )
 
         def ld_xw():
@@ -159,11 +169,11 @@ def tile_cossim2d_v_kernel(tc, x, w, p, q, x_rnorm, w_rnorm, sim, grad_out, out_
             xw4 = xw[:].rearrange("p r (a m) -> p r a m", a=2)
             for yh in range(2):
                 for a in range(2):
-                    for b in range(NB):
-                        p0 = 64 * yh + 8 * b
-                        nc.sync.dma_start(
-                            out=xw4[p0 : p0 + 8, :, a, :],
-                            in_=x[b, 2 * yh : 2 * yh + 16, 2 * a : 2 * a + 16, :].rearrange("r (zw e) c -> zw r (e c)", e=2),
+                    for zw in range(8):
+                        v0 = 2 * a + 2 * zw
+                        nc.gpsimd.dma_start(
+                            out=xw4[64 * yh + zw : 64 * yh + 64 : 8, :, a, :],
+                            in_=x[:, 2 * yh : 2 * yh + 16, v0 : v0 + 2, :].rearrange("b r e c -> b r (e c)"),
                         )
 
         def small_consts():
@@ -222,11 +232,11 @@ def tile_cossim2d_v_kernel(tc, x, w, p, q, x_rnorm, w_rnorm, sim, grad_out, out_
         def a_step(c, yy):
             s_sb = sims[c]
             lg = logs[c]
-            off = chunk_off(yy)
+            off = 128 * yy
             for g in range(2):
                 ps = bank("ts")
                 for t in range(4):
-                    nc.tensor.transpose(ps[:, t * 128 : (t + 1) * 128], s_sb[:, yy, 512 * g + t : 512 * (g + 1) : 4], ident[:])
+                    nc.tensor.transpose(ps[:, t * 128 : (t + 1) * 128], s_sb[:, yy, 512 * g + t : 512 * (g + 1) : 4], perm[:])
                 nc.scalar.activation(
                     out=lg[:, 4 * g : 4 * g + 4, off : off + 128],
                     in_=ps[:].rearrange("p (t c) -> p t c", t=4),
@@ -238,8 +248,8 @@ def tile_cossim2d_v_kernel(tc, x, w, p, q, x_rnorm, w_rnorm, sim, grad_out, out_
             lg = logs[c]
             nc.scalar.activation(out=lg[:, k, :], in_=lg[:, k, :], func=ACT.Exp, bias=lne_c[:, k : k + 1], scale=em1_c[:, k : k + 1])
 
-        def new_plain(c):
-            plains[c] = big.tile([P, 8, 512], BF16, name="pl%d" % c, offset=O_PL[c % 2], align_bytes=64)
+        def new_plain(hh):
+            plains[hh] = big.tile([P, 8, 1024], BF16, name="pl%d" % hh, offset=O_PL[0], align_bytes=64)
 
         gts = {}
 
@@ -249,19 +259,15 @@ def tile_cossim2d_v_kernel(tc, x, w, p, q, x_rnorm, w_rnorm, sim, grad_out, out_
             gts[(c, yy)] = ps
             for gh in range(4):
                 c0 = yy * 512 + 256 * (gh // 2)
-                nc.tensor.transpose(ps[:, gh * 128 : (gh + 1) * 128], gw[:, c0 + gh % 2 : c0 + 256 : 2], ident[:])
+                nc.tensor.transpose(ps[:, gh * 128 : (gh + 1) * 128], gw[:, c0 + gh % 2 : c0 + 256 : 2], perm[:])
 
         def m_v(c, yy):
-            pl = plains[c]
-            lg = logs[c]
-            off = chunk_off(yy)
-            ps = gts[(c, yy)]
-            nc.vector.tensor_tensor(
-                out=pl[:, :, off : off + 128].rearrange("p (k e) c -> p k e c", e=2),
-                in0=lg[:, :, off : off + 128].rearrange("p (k e) c -> p k e c", e=2),
-                in1=ps[:].bitcast(BF16).rearrange("p (k c e) -> p k e c", k=4, e=2),
-                op=ALU.mult,
-            )
+            b = 4 * (c % 2) + yy
+            pl6 = plains[c // 2][:].rearrange("p (k e) (r b z) -> p k e r b z", e=2, r=8, b=NB)
+            lg5 = logs[c][:, :, 128 * yy : 128 * yy + 128].rearrange("p (k e) (r z) -> p k e r z", e=2, r=8)
+            ps5 = gts[(c, yy)][:].bitcast(BF16).rearrange("p (k r z e) -> p k e r z", k=4, r=8, e=2)
+            for e in range(2):
+                nc.vector.tensor_tensor(out=pl6[:, :, e, :, b, :], in0=lg5[:, :, e], in1=ps5[:, :, e], op=ALU.mult)
 
         def u_copy(c, g):
             if g == 0:
@@ -270,11 +276,14 @@ def tile_cossim2d_v_kernel(tc, x, w, p, q, x_rnorm, w_rnorm, sim, grad_out, out_
                 ucodes[c] = [uc, us, None, None]
             uf = big.tile([P, 512, 4], BF16, name="uf%d_%d" % (c, g), offset=O_UF[g], align_bytes=64)
             ucodes[c][2 + g] = uf
-            src = plains[c][:, 4 * g : 4 * g + 4, :].rearrange("p t c -> p c t")
-            if (c, g) in U_ON_SCALAR:
-                nc.scalar.copy(out=uf[:], in_=src)
-            else:
-                nc.vector.tensor_copy(out=uf[:], in_=src)
+            for yy in range(4):
+                s0 = (yy % 2) * 512 + (2 * (c % 2) + yy // 2) * 128
+                src = plains[c // 2][:, 4 * g : 4 * g + 4, s0 : s0 + 128].rearrange("p t (b z) -> p z b t", b=NB)
+                dst = uf[:, chunk_off(yy) : chunk_off(yy) + 128, :].rearrange("p (z b) t -> p z b t", b=NB)
+                if (c, g) in U_ON_SCALAR:
+                    nc.scalar.copy(out=dst, in_=src)
+                else:
+                    nc.vector.tensor_copy(out=dst, in_=src)
 
         def u_quant(c, g):
             uc, us = ucodes[c][0], ucodes[c][1]
@@ -284,12 +293,12 @@ def tile_cossim2d_v_kernel(tc, x, w, p, q, x_rnorm, w_rnorm, sim, grad_out, out_
         def t_step(c, kp):
             if kp == 0:
                 tfs[c] = big.tile([P, U, 4], BF16, name="tf%d" % c, offset=O_TF, align_bytes=64)
-            plw = plains[c][:].rearrange("p k c -> p (k c)").bitcast(F32)
+            plw = plains[c // 2][:].rearrange("p k c -> p (k c)").bitcast(F32)
             tfw = tfs[c][:].rearrange("p u t -> p (u t)").bitcast(F32).rearrange("p (u l) -> p u l", l=2)
             ps = bank("ts")
             for l in range(2):
                 for kk in range(2):
-                    c0 = (2 * kp + kk) * 256 + l * 128
+                    c0 = (2 * kp + kk) * 512 + l * 256 + (c % 2) * 128
                     nc.tensor.transpose(ps[:, l * 256 + kk * 128 : l * 256 + (kk + 1) * 128], plw[:, c0 : c0 + 128], ident[:])
             nc.scalar.copy(out=tfw[:, kp * 256 : (kp + 1) * 256, :], in_=ps[:].rearrange("p (l c) -> p c l", l=2))
 
@@ -364,23 +373,23 @@ def tile_cossim2d_v_kernel(tc, x, w, p, q, x_rnorm, w_rnorm, sim, grad_out, out_
         ld_w()
         ld_sim(0)
         ld_sim(1)
+        ld_xc()
+        ld_rx()
         small_consts()
         w_turn()
         ld_go(0)
-        ld_rx()
-        ld_xc()
         ld_go(1)
         new_log(0)
-        for yy in range(4):
-            v_abs(0, yy)
-            a_step(0, yy)
+        for bb in range(4):
+            v_abs(0, bb)
+            a_step(0, bb)
         w_scale()
         for k in range(8):
             e_step(0, k)
         m_pe(0, 0)
         m_pe(0, 1)
-        for yy in range(4):
-            v_abs(1, yy)
+        for bb in range(4):
+            v_abs(1, bb)
         new_log(1)
         a_step(1, 0)
         ld_sim(2)
@@ -390,33 +399,18 @@ def tile_cossim2d_v_kernel(tc, x, w, p, q, x_rnorm, w_rnorm, sim, grad_out, out_
         m_pe(0, 2)
         m_v(0, 1)
         m_pe(0, 3)
-        for yy in range(1, 4):
-            a_step(1, yy)
+        for bb in range(1, 4):
+            a_step(1, bb)
         m_v(0, 2)
         m_v(0, 3)
+        for k in range(8):
+            e_step(1, k)
         ld_sim(3)
         ld_go(2)
-        for g in range(2):
-            u_copy(0, g)
-        for kp in range(4):
-            t_step(0, kp)
-        for g in range(2):
-            u_quant(0, g)
-        t_quant(0)
+        for bb in range(4):
+            v_abs(2, bb)
         m_pe(1, 0)
         m_pe(1, 1)
-        new_log(2)
-        for yy in range(4):
-            if yy < 2:
-                for k in range(4 * yy, 4 * yy + 4):
-                    e_step(1, k)
-                v_abs(2, 2 * yy)
-                v_abs(2, 2 * yy + 1)
-            x_step(0, yy)
-            if yy >= 2:
-                a_step(2, 2 * yy - 4)
-                a_step(2, 2 * yy - 3)
-        new_plain(1)
         m_v(1, 0)
         m_pe(1, 2)
         m_v(1, 1)
@@ -424,20 +418,31 @@ def tile_cossim2d_v_kernel(tc, x, w, p, q, x_rnorm, w_rnorm, sim, grad_out, out_
         m_v(1, 2)
         m_v(1, 3)
         ld_go(3)
-        ld_xw()
         for k in range(8):
             later.append((w_squares, (k,)))
         for h in range(NH):
             later.append((x_squares, (h,)))
-        for yy in range(4):
-            v_abs(3, yy)
+        new_log(2)
+        for bb in range(4):
+            a_step(2, bb)
+        ld_xw()
+        for g in range(2):
+            u_copy(0, g)
         for kp in range(4):
-            t_step(1, kp)
+            t_step(0, kp)
+        for bb in range(4):
+            v_abs(3, bb)
+        for g in range(2):
+            u_quant(0, g)
+        t_quant(0)
         new_log(3)
         for yy in range(4):
+            x_step(0, yy)
             a_step(3, yy)
         for g in range(2):
             u_copy(1, g)
+        for kp in range(4):
+            t_step(1, kp)
         for g in range(2):
             u_quant(1, g)
         t_quant(1)
@@ -445,51 +450,45 @@ def tile_cossim2d_v_kernel(tc, x, w, p, q, x_rnorm, w_rnorm, sim, grad_out, out_
         m_pe(2, 1)
         for yy in range(4):
             x_step(1, yy)
-            e_step(2, 2 * yy)
-            e_step(2, 2 * yy + 1)
-        new_plain(2)
-        m_v(2, 0)
-        m_pe(2, 2)
-        m_v(2, 1)
-        m_pe(2, 3)
-        m_v(2, 2)
-        m_v(2, 3)
-        for k in range(8):
-            e_step(3, k)
+            for k in range(4 * (yy % 2), 4 * (yy % 2) + 4):
+                e_step(2 + yy // 2, k)
+        fill(6)
+        new_plain(1)
+        for c in (2, 3):
+            if c == 3:
+                m_pe(3, 0)
+                m_pe(3, 1)
+            m_v(c, 0)
+            m_pe(c, 2)
+            m_v(c, 1)
+            m_pe(c, 3)
+            m_v(c, 2)
+            m_v(c, 3)
         for g in range(2):
             u_copy(2, g)
         for kp in range(4):
             t_step(2, kp)
-        fill(6)
-        m_pe(3, 0)
-        m_pe(3, 1)
+        n_scale(0)
         for g in range(2):
             u_quant(2, g)
         t_quant(2)
-        new_plain(3)
-        m_v(3, 0)
-        m_pe(3, 2)
-        m_v(3, 1)
-        m_pe(3, 3)
-        m_v(3, 2)
-        m_v(3, 3)
-        for g in range(2):
-            u_copy(3, g)
-        for kp in range(4):
-            t_step(3, kp)
-        n_scale(0)
         n_scale(1)
         for c in range(2):
             for i in range(3):
                 later.insert(3 * c + i, (n_copy, (c, i)))
         for yy in range(4):
             x_step(2, yy)
-            fill(1)
-            if yy == 1:
+            if yy < 2:
+                u_copy(3, yy)
+                t_step(3, 2 * yy)
+                t_step(3, 2 * yy + 1)
+            else:
+                fill(1)
+            if yy == 2:
                 for g in range(2):
                     u_quant(3, g)
                 t_quant(3)
-        fill(2)
+        fill(4)
         n_quant(0)
         for yy in range(4):
             x_step(3, yy)
@@ -574,17 +573,16 @@ def tile_cossim2d_v_kernel(tc, x, w, p, q, x_rnorm, w_rnorm, sim, grad_out, out_
         def park():
             nc.sync.dma_start(out=park0, in_=ha4[:, :, 0, :])
             nc.sync.dma_start(out=park2, in_=ha4[:, :, 2, :])
-            nc.sync.dma_start(out=out_0[:, :, 0, :], in_=ha4[0:P:16, :, 0, :])
-            nc.sync.dma_start(out=out_0[:, :, 17, :], in_=ha4[15:P:16, :, 2, :])
-            for b in range(NB):
-                nc.sync.dma_start(out=r0[16 * b : 16 * b + 15], in_=park0[16 * b + 1 : 16 * b + 16])
-                nc.sync.dma_start(out=r2[16 * b + 1 : 16 * b + 16], in_=park2[16 * b : 16 * b + 15])
+            nc.sync.dma_start(out=out_0[:, :, 0, :], in_=ha4[0:8, :, 0, :])
+            nc.sync.dma_start(out=out_0[:, :, 17, :], in_=ha4[120:128, :, 2, :])
+            nc.sync.dma_start(out=r0[0:120], in_=park0[8:128])
+            nc.sync.dma_start(out=r2[8:128], in_=park2[0:120])
 
         def x_finish():
             nc.gpsimd.tensor_tensor(out=r0[:], in0=r0[:], in1=ha4[:, :, 1, :], op=ALU.add)
             nc.gpsimd.tensor_tensor(out=r0[:], in0=r0[:], in1=r2[:], op=ALU.add)
             for b in range(NB):
-                nc.gpsimd.dma_start(out=out_0[b, :, 1:17, :].rearrange("h v c -> v h c"), in_=r0[16 * b : 16 * b + 16])
+                nc.gpsimd.dma_start(out=out_0[b, :, 1:17, :].rearrange("h v c -> v h c"), in_=r0[b:P:8])
 
         def w_coef(k):
             nc.vector.tensor_reduce(out=cw[:, k : k + 1], in_=cw_p[:, k, :], axis=AX.X, op=ALU.add)

@@ -24,7 +24,7 @@ T = 2048
 FLOPS = 2 * 2 * T * D * U
 
 DX_WINDOWS = ((0, 0), (384, 0), (640, 128))
-DW_WINDOWS = ((0, 0, 512, 0), (512, 0, 512, 512), (640, 384, 128, 1024))
+DW_WINDOWS = ((0, 0, 512, 0), (512, 0, 512, 512))
 
 O_DTC = 0
 O_DTS = 16384
@@ -36,7 +36,7 @@ O_WNS = 89600
 O_SIM = (91904, 108288)
 O_LG = (124672, 141056)
 O_GO = (157440, 165632)
-O_UF = (173824, 177920)
+O_UF = (173824, 177920, 221696, 225792)
 O_PL = (182016, 190208)
 O_UC = (198400, 202496)
 O_US = (206592, 207616)
@@ -147,19 +147,21 @@ def tile_cossim2d_v_kernel(tc, x, w, p, q, x_rnorm, w_rnorm, sim, grad_out, out_
                     in_=grad_out[4 * bq + 2 * b2 : 4 * bq + 2 * b2 + 2, 8 * hh : 8 * hh + 8].rearrange("b y z u -> (y z) b u"),
                 )
 
-        def ld_xc():
+        def ld_xc(js):
             xc4 = xc[:].rearrange("p h (j c) -> p h j c", j=3)
-            for j in range(3):
+            for j in js:
                 for b in range(NB):
-                    nc.scalar.dma_start(out=xc4[b:P:8, :, j, :], in_=x[b, :, j : j + 16, :].rearrange("h v c -> v h c"))
+                    nc.gpsimd.dma_start(out=xc4[b:P:8, :, j, :], in_=x[b, :, j : j + 16, :].rearrange("h v c -> v h c"))
 
-        def ld_rx():
+        def ld_rxc():
             with nc.allow_non_contiguous_dma(reason="2048 single floats, once"):
                 for b in range(NB):
-                    nc.scalar.dma_start(out=rx_c[b:P:8, :], in_=x_rnorm[b].rearrange("y z -> z y"))
+                    nc.sync.dma_start(out=rx_c[b:P:8, :], in_=x_rnorm[b].rearrange("y z -> z y"))
+
+        def ld_rxt():
             for yh in range(2):
                 for zw in range(8):
-                    nc.scalar.dma_start(
+                    nc.sync.dma_start(
                         out=rx_t[64 * yh + zw : 64 * yh + 64 : 8, :, :], in_=x_rnorm[:, 2 * yh : 2 * yh + 14, 2 * zw : 2 * zw + 2]
                     )
 
@@ -171,7 +173,7 @@ def tile_cossim2d_v_kernel(tc, x, w, p, q, x_rnorm, w_rnorm, sim, grad_out, out_
                 for a in range(2):
                     for zw in range(8):
                         v0 = 2 * a + 2 * zw
-                        nc.gpsimd.dma_start(
+                        nc.sync.dma_start(
                             out=xw4[64 * yh + zw : 64 * yh + 64 : 8, :, a, :],
                             in_=x[:, 2 * yh : 2 * yh + 16, v0 : v0 + 2, :].rearrange("b r e c -> b r (e c)"),
                         )
@@ -274,16 +276,13 @@ def tile_cossim2d_v_kernel(tc, x, w, p, q, x_rnorm, w_rnorm, sim, grad_out, out_
                 uc = big.tile([P, 2, 512], U32, name="uc%d" % c, offset=O_UC[c % 2], align_bytes=64)
                 us = big.tile([P, 2, 512], U8, name="us%d" % c, offset=O_US[c % 2], align_bytes=64)
                 ucodes[c] = [uc, us, None, None]
-            uf = big.tile([P, 512, 4], BF16, name="uf%d_%d" % (c, g), offset=O_UF[g], align_bytes=64)
+            uf = big.tile([P, 512, 4], BF16, name="uf%d_%d" % (c, g), offset=O_UF[2 * (c % 2) + g], align_bytes=64)
             ucodes[c][2 + g] = uf
             for yy in range(4):
                 s0 = (yy % 2) * 512 + (2 * (c % 2) + yy // 2) * 128
                 src = plains[c // 2][:, 4 * g : 4 * g + 4, s0 : s0 + 128].rearrange("p t (b z) -> p z b t", b=NB)
                 dst = uf[:, chunk_off(yy) : chunk_off(yy) + 128, :].rearrange("p (z b) t -> p z b t", b=NB)
-                if (c, g) in U_ON_SCALAR:
-                    nc.scalar.copy(out=dst, in_=src)
-                else:
-                    nc.vector.tensor_copy(out=dst, in_=src)
+                nc.gpsimd.tensor_scalar(out=dst, in0=src, scalar1=1.0, scalar2=0.0, op0=ALU.mult, op1=ALU.add)
 
         def u_quant(c, g):
             uc, us = ucodes[c][0], ucodes[c][1]
@@ -356,7 +355,7 @@ def tile_cossim2d_v_kernel(tc, x, w, p, q, x_rnorm, w_rnorm, sim, grad_out, out_
             if c in N_ON_SCALAR:
                 nc.scalar.copy(out=xi[:, 384 * i : 384 * (i + 1), :], in_=src)
             else:
-                nc.vector.tensor_copy(out=xi[:, 384 * i : 384 * (i + 1), :], in_=src)
+                nc.gpsimd.tensor_scalar(out=xi[:, 384 * i : 384 * (i + 1), :], in0=src, scalar1=1.0, scalar2=0.0, op0=ALU.mult, op1=ALU.add)
 
         def n_quant(c):
             xif = xts[("i", c)][:].rearrange("p d t -> p (d t)")
@@ -373,17 +372,18 @@ def tile_cossim2d_v_kernel(tc, x, w, p, q, x_rnorm, w_rnorm, sim, grad_out, out_
         ld_w()
         ld_sim(0)
         ld_sim(1)
-        ld_xc()
-        ld_rx()
+        ld_xc((0,))
         small_consts()
         w_turn()
         ld_go(0)
         ld_go(1)
+        ld_rxc()
         new_log(0)
         for bb in range(4):
             v_abs(0, bb)
             a_step(0, bb)
         w_scale()
+        ld_xc((1, 2))
         for k in range(8):
             e_step(0, k)
         m_pe(0, 0)
@@ -426,6 +426,7 @@ def tile_cossim2d_v_kernel(tc, x, w, p, q, x_rnorm, w_rnorm, sim, grad_out, out_
         for bb in range(4):
             a_step(2, bb)
         ld_xw()
+        ld_rxt()
         for g in range(2):
             u_copy(0, g)
         for kp in range(4):
@@ -490,21 +491,17 @@ def tile_cossim2d_v_kernel(tc, x, w, p, q, x_rnorm, w_rnorm, sim, grad_out, out_
                 t_quant(3)
         fill(4)
         n_quant(0)
+        n_scale(2)
+        for i in range(3):
+            n_copy(2, i)
         for yy in range(4):
             x_step(3, yy)
-            fill(1 if yy == 0 else 3)
+            fill(5)
             if yy == 0:
-                n_scale(2)
-                for i in range(3):
-                    n_copy(2, i)
-            if yy == 1:
                 n_quant(1)
-                n_quant(2)
-            if yy == 2:
                 n_scale(3)
                 for i in range(3):
                     n_copy(3, i)
-        n_quant(3)
         fill(len(later))
 
         sx = keep.tile([P, NY], F32, name="sx")
@@ -524,11 +521,9 @@ def tile_cossim2d_v_kernel(tc, x, w, p, q, x_rnorm, w_rnorm, sim, grad_out, out_
         park2 = flat1[P * NH * 128 : 2 * P * NH * 128].rearrange("(p h c) -> p h c", p=P, c=128)
 
         def dw_mm(k):
-            res = []
-            for wi in range(3):
+            for wi in range(2):
                 ws = DW_WINDOWS[wi][0]
                 ps = bank("mm")
-                res.append(ps)
                 for c in range(4):
                     nc.tensor.matmul_mx(
                         out=ps[:],
@@ -545,6 +540,31 @@ def tile_cossim2d_v_kernel(tc, x, w, p, q, x_rnorm, w_rnorm, sim, grad_out, out_
                     op0=ALU.mult, op1=ALU.mult, accum_out=cw_p[:, k, wi : wi + 1],
                 )
                 nc.scalar.activation(out=f1[:, k, d0 : d0 + n], in_=ps[:, uo : uo + n], func=ACT.Copy, scale=rw_c[:, k : k + 1])
+
+        def dw_last(g):
+            ps = bank("mm")
+            for c in range(4):
+                nc.tensor.matmul_mx(
+                    out=ps[:],
+                    lhsT=xn_codes[:, c, 1024:D].bitcast(E4),
+                    lhsT_scale=xn_scales[:, c, 1024:D],
+                    rhs=dt_codes[:, c, 512 * g : 512 * (g + 1)].bitcast(E5),
+                    rhs_scale=dt_scales[:, c, 512 * g : 512 * (g + 1)],
+                    start=(c == 0),
+                    stop=(c == 3),
+                )
+            d8 = big.tile([P, 512], F32, name="d8_%d" % g, offset=O_OT[g], align_bytes=64)
+            nc.scalar.copy(out=d8[:], in_=ps[:])
+            ps2 = bank("ts")
+            for t in range(4):
+                nc.tensor.transpose(ps2[:, t * 128 : (t + 1) * 128], d8[:, t * 128 : (t + 1) * 128], ident[:])
+            for t in range(4):
+                k = 4 * g + t
+                nc.vector.scalar_tensor_tensor(
+                    out=junk_c[:, 0:128], in0=ps2[:, t * 128 : (t + 1) * 128], scalar=1.0, in1=wt[:, g, 1024:D, t],
+                    op0=ALU.mult, op1=ALU.mult, accum_out=cw_p[:, k, 2:3],
+                )
+                nc.scalar.activation(out=f1[:, k, 1024:D], in_=ps2[:, t * 128 : (t + 1) * 128], func=ACT.Copy, scale=rw_c[:, k : k + 1])
 
         def x_factors():
             nc.vector.tensor_tensor(out=sx[:], in0=rs_c[:, 0:16], in1=rs_c[:, 1:17], op=ALU.add)
@@ -594,23 +614,29 @@ def tile_cossim2d_v_kernel(tc, x, w, p, q, x_rnorm, w_rnorm, sim, grad_out, out_
             )
 
         def w_store(g, kd, n):
-            ps = bank("ts")
+            ps = bank("ts" if n % 2 == 0 else "tv")
             for t in range(4):
                 nc.tensor.transpose(ps[:, t * 128 : (t + 1) * 128], f1[:, 4 * g + t, kd * 128 : (kd + 1) * 128], ident[:])
             ot = big.tile([P, 512], F32, name="ot%d_%d" % (g, kd), offset=O_OT[n % 4], align_bytes=64)
-            nc.scalar.copy(out=ot[:].rearrange("p (u t) -> p u t", t=4), in_=ps[:].rearrange("p (t u) -> p u t", t=4))
+            if g == 1 and n % 2 == 1:
+                nc.vector.tensor_copy(out=ot[:].rearrange("p (u t) -> p u t", t=4), in_=ps[:].rearrange("p (t u) -> p u t", t=4))
+            else:
+                nc.scalar.copy(out=ot[:].rearrange("p (u t) -> p u t", t=4), in_=ps[:].rearrange("p (t u) -> p u t", t=4))
             nc.sync.dma_start(out=out_1[0, kd * 128 : (kd + 1) * 128, 512 * g : 512 * (g + 1)], in_=ot[:])
 
         nc.gpsimd.memset(r0[:], 0.0)
         nc.gpsimd.memset(r2[:], 0.0)
-        w_factors()
         x_factors()
+        for h in range(NH):
+            x_norm_term(h)
+        park()
+        x_finish()
+        n_quant(2)
+        n_quant(3)
+        w_factors()
+        dw_last(0)
+        dw_last(1)
         for k in range(4):
-            for h in range(9 * k, min(9 * k + 9, NH)):
-                x_norm_term(h)
-            if k == 2:
-                park()
-                x_finish()
             dw_mm(k)
             w_coef(k)
             w_final(k)

@@ -49,8 +49,8 @@ O_WSB = 157440
 O_WN = 34304
 O_JW = 194304
 O_F1 = 91904
-O_R0 = 128768
-O_R2 = 137984
+O_R0 = 182016
+O_R2 = 191232
 O_OT = (147200, 149248, 151296, 153344)
 O_JC = 155392
 O_JW2 = 219392
@@ -151,7 +151,7 @@ def tile_cossim2d_v_kernel(tc, x, w, p, q, x_rnorm, w_rnorm, sim, grad_out, out_
             xc4 = xc[:].rearrange("p h (j c) -> p h j c", j=3)
             for j in js:
                 for b in range(NB):
-                    nc.gpsimd.dma_start(out=xc4[b:P:8, :, j, :], in_=x[b, :, j : j + 16, :].rearrange("h v c -> v h c"))
+                    nc.sync.dma_start(out=xc4[b:P:8, :, j, :], in_=x[b, :, j : j + 16, :].rearrange("h v c -> v h c"))
 
         def ld_rxc():
             with nc.allow_non_contiguous_dma(reason="2048 single floats, once"):
@@ -203,7 +203,7 @@ def tile_cossim2d_v_kernel(tc, x, w, p, q, x_rnorm, w_rnorm, sim, grad_out, out_
         wn = big.tile([P, 2, D, 4], BF16, name="wn", offset=O_WN, align_bytes=64)
 
         def w_scale():
-            for g, eng in ((0, nc.gpsimd), (1, nc.vector)):
+            for g, eng in ((0, nc.vector), (1, nc.vector)):
                 eng.tensor_tensor(
                     out=wn[:, g], in0=wt[:, g], in1=rw_c[:, 4 * g : 4 * g + 4].unsqueeze(1).to_broadcast([P, D, 4]), op=ALU.mult
                 )
@@ -372,7 +372,6 @@ def tile_cossim2d_v_kernel(tc, x, w, p, q, x_rnorm, w_rnorm, sim, grad_out, out_
         ld_w()
         ld_sim(0)
         ld_sim(1)
-        ld_xc((0,))
         small_consts()
         w_turn()
         ld_go(0)
@@ -383,7 +382,6 @@ def tile_cossim2d_v_kernel(tc, x, w, p, q, x_rnorm, w_rnorm, sim, grad_out, out_
             v_abs(0, bb)
             a_step(0, bb)
         w_scale()
-        ld_xc((1, 2))
         for k in range(8):
             e_step(0, k)
         m_pe(0, 0)
@@ -393,6 +391,7 @@ def tile_cossim2d_v_kernel(tc, x, w, p, q, x_rnorm, w_rnorm, sim, grad_out, out_
         new_log(1)
         a_step(1, 0)
         ld_sim(2)
+        ld_xc((0, 1, 2))
         w_quant()
         new_plain(0)
         m_v(0, 0)
@@ -494,9 +493,14 @@ def tile_cossim2d_v_kernel(tc, x, w, p, q, x_rnorm, w_rnorm, sim, grad_out, out_
         n_scale(2)
         for i in range(3):
             n_copy(2, i)
+        r0 = big.tile([P, NH, 128], F32, name="r0", offset=O_R0, align_bytes=64)
+        r2 = big.tile([P, NH, 128], F32, name="r2", offset=O_R2, align_bytes=64)
         for yy in range(4):
             x_step(3, yy)
             fill(5)
+            if yy == 1:
+                nc.gpsimd.memset(r0[:], 0.0)
+                nc.gpsimd.memset(r2[:], 0.0)
             if yy == 0:
                 n_quant(1)
                 n_scale(3)
@@ -513,8 +517,6 @@ def tile_cossim2d_v_kernel(tc, x, w, p, q, x_rnorm, w_rnorm, sim, grad_out, out_
         cw = keep.tile([P, 8], F32, name="cw")
         f1 = big.tile([P, 8, D], F32, name="f1", offset=O_F1, align_bytes=64)
         junk_c = big.tile([P, 512], F32, name="junk_c", offset=O_JC, align_bytes=64)
-        r0 = big.tile([P, NH, 128], F32, name="r0", offset=O_R0, align_bytes=64)
-        r2 = big.tile([P, NH, 128], F32, name="r2", offset=O_R2, align_bytes=64)
         ha4 = ha[:].rearrange("p h (j c) -> p h j c", j=3)
         flat1 = out_1.rearrange("o d u -> (o d u)")
         park0 = flat1[0 : P * NH * 128].rearrange("(p h c) -> p h c", p=P, c=128)
@@ -599,10 +601,10 @@ def tile_cossim2d_v_kernel(tc, x, w, p, q, x_rnorm, w_rnorm, sim, grad_out, out_
             nc.sync.dma_start(out=r2[8:128], in_=park2[0:120])
 
         def x_finish():
-            nc.gpsimd.tensor_tensor(out=r0[:], in0=r0[:], in1=ha4[:, :, 1, :], op=ALU.add)
-            nc.gpsimd.tensor_tensor(out=r0[:], in0=r0[:], in1=r2[:], op=ALU.add)
+            nc.vector.tensor_tensor(out=r0[:], in0=r0[:], in1=ha4[:, :, 1, :], op=ALU.add)
+            nc.vector.tensor_tensor(out=r0[:], in0=r0[:], in1=r2[:], op=ALU.add)
             for b in range(NB):
-                nc.gpsimd.dma_start(out=out_0[b, :, 1:17, :].rearrange("h v c -> v h c"), in_=r0[b:P:8])
+                nc.sync.dma_start(out=out_0[b, :, 1:17, :].rearrange("h v c -> v h c"), in_=r0[b:P:8])
 
         def w_coef(k):
             nc.vector.tensor_reduce(out=cw[:, k : k + 1], in_=cw_p[:, k, :], axis=AX.X, op=ALU.add)
@@ -624,13 +626,10 @@ def tile_cossim2d_v_kernel(tc, x, w, p, q, x_rnorm, w_rnorm, sim, grad_out, out_
                 nc.scalar.copy(out=ot[:].rearrange("p (u t) -> p u t", t=4), in_=ps[:].rearrange("p (t u) -> p u t", t=4))
             nc.sync.dma_start(out=out_1[0, kd * 128 : (kd + 1) * 128, 512 * g : 512 * (g + 1)], in_=ot[:])
 
-        nc.gpsimd.memset(r0[:], 0.0)
-        nc.gpsimd.memset(r2[:], 0.0)
         x_factors()
         for h in range(NH):
             x_norm_term(h)
         park()
-        x_finish()
         n_quant(2)
         n_quant(3)
         w_factors()
@@ -640,6 +639,8 @@ def tile_cossim2d_v_kernel(tc, x, w, p, q, x_rnorm, w_rnorm, sim, grad_out, out_
             dw_mm(k)
             w_coef(k)
             w_final(k)
+            if k == 1:
+                x_finish()
         for k in range(4, 8):
             dw_mm(k)
             w_coef(k)

@@ -45,13 +45,13 @@ O_JV = 216832
 O_JS = 218368
 O_XNC = 157440
 O_XNS = 175872
-O_WSB = 157440
+O_WSB = 0
 O_WN = 34304
 O_JW = 194304
 O_F1 = 91904
 O_R0 = 182016
 O_R2 = 191232
-O_OT = (147200, 149248, 151296, 153344)
+O_OT = (128768, 130816, 132864, 134912, 136960, 139008, 141056, 143104)
 O_JC = 155392
 O_JW2 = 219392
 O_XI = (108288, 117504)
@@ -184,12 +184,11 @@ def tile_cossim2d_v_kernel(tc, x, w, p, q, x_rnorm, w_rnorm, sim, grad_out, out_
             nc.scalar.activation(out=lne_c[:], in_=e_c[:], func=ACT.Ln)
             nc.scalar.activation(out=qq_c[:], in_=q_c[:], func=ACT.Square, scale=1.0 / 0.3)
 
-        def w_turn():
+        def w_turn(k0):
             ww = w_sb[:].rearrange("p k u -> p (k u)").bitcast(F32)
             wtw = wt[:].rearrange("p g d t -> p (g d t)").bitcast(F32).rearrange("p (g d h) -> p g d h", g=2, h=2)
             for g in range(2):
-                for k0 in range(0, 9, 2):
-                    nk = min(2, 9 - k0)
+                for nk in (min(2, 9 - k0),):
                     ps = bank("ts")
                     for h in range(2):
                         for kk in range(nk):
@@ -202,10 +201,12 @@ def tile_cossim2d_v_kernel(tc, x, w, p, q, x_rnorm, w_rnorm, sim, grad_out, out_
 
         wn = big.tile([P, 2, D, 4], BF16, name="wn", offset=O_WN, align_bytes=64)
 
-        def w_scale():
-            for g, eng in ((0, nc.vector), (1, nc.vector)):
-                eng.tensor_tensor(
-                    out=wn[:, g], in0=wt[:, g], in1=rw_c[:, 4 * g : 4 * g + 4].unsqueeze(1).to_broadcast([P, D, 4]), op=ALU.mult
+        def w_scale(k0):
+            d0, d1 = 128 * k0, min(128 * (k0 + 2), D)
+            for g in range(2):
+                nc.vector.tensor_tensor(
+                    out=wn[:, g, d0:d1], in0=wt[:, g, d0:d1],
+                    in1=rw_c[:, 4 * g : 4 * g + 4].unsqueeze(1).to_broadcast([P, d1 - d0, 4]), op=ALU.mult,
                 )
 
         def w_quant():
@@ -257,7 +258,7 @@ def tile_cossim2d_v_kernel(tc, x, w, p, q, x_rnorm, w_rnorm, sim, grad_out, out_
 
         def m_pe(c, yy):
             gw = gos[c][:].rearrange("p y u -> p (y u)").bitcast(F32)
-            ps = bank("tv")
+            ps = bank("mm" if c < 2 and yy >= 2 else "tv")
             gts[(c, yy)] = ps
             for gh in range(4):
                 c0 = yy * 512 + 256 * (gh // 2)
@@ -282,7 +283,10 @@ def tile_cossim2d_v_kernel(tc, x, w, p, q, x_rnorm, w_rnorm, sim, grad_out, out_
                 s0 = (yy % 2) * 512 + (2 * (c % 2) + yy // 2) * 128
                 src = plains[c // 2][:, 4 * g : 4 * g + 4, s0 : s0 + 128].rearrange("p t (b z) -> p z b t", b=NB)
                 dst = uf[:, chunk_off(yy) : chunk_off(yy) + 128, :].rearrange("p (z b) t -> p z b t", b=NB)
-                nc.gpsimd.tensor_scalar(out=dst, in0=src, scalar1=1.0, scalar2=0.0, op0=ALU.mult, op1=ALU.add)
+                if c % 2 == 1:
+                    nc.gpsimd.tensor_scalar(out=dst, in0=src, scalar1=1.0, scalar2=0.0, op0=ALU.mult, op1=ALU.add)
+                else:
+                    nc.vector.tensor_copy(out=dst, in_=src)
 
         def u_quant(c, g):
             uc, us = ucodes[c][0], ucodes[c][1]
@@ -372,50 +376,45 @@ def tile_cossim2d_v_kernel(tc, x, w, p, q, x_rnorm, w_rnorm, sim, grad_out, out_
         ld_w()
         ld_sim(0)
         ld_sim(1)
-        small_consts()
-        w_turn()
         ld_go(0)
         ld_go(1)
         ld_rxc()
+        small_consts()
+        for k0 in range(0, 9, 2):
+            w_turn(k0)
         new_log(0)
+        w_scale(0)
+        w_scale(2)
         for bb in range(4):
             v_abs(0, bb)
             a_step(0, bb)
-        w_scale()
-        for k in range(8):
-            e_step(0, k)
-        m_pe(0, 0)
-        m_pe(0, 1)
+            if bb < 3:
+                w_scale(4 + 2 * bb)
         for bb in range(4):
             v_abs(1, bb)
         new_log(1)
-        a_step(1, 0)
+        for bb in range(4):
+            a_step(1, bb)
+        for k in range(8):
+            e_step(0, k)
+        for bb in range(4):
+            m_pe(0, bb)
         ld_sim(2)
+        ld_sim(3)
         ld_xc((0, 1, 2))
         w_quant()
-        new_plain(0)
-        m_v(0, 0)
-        m_pe(0, 2)
-        m_v(0, 1)
-        m_pe(0, 3)
-        for bb in range(1, 4):
-            a_step(1, bb)
-        m_v(0, 2)
-        m_v(0, 3)
-        for k in range(8):
-            e_step(1, k)
-        ld_sim(3)
-        ld_go(2)
         for bb in range(4):
             v_abs(2, bb)
-        m_pe(1, 0)
-        m_pe(1, 1)
-        m_v(1, 0)
-        m_pe(1, 2)
-        m_v(1, 1)
-        m_pe(1, 3)
-        m_v(1, 2)
-        m_v(1, 3)
+        new_plain(0)
+        for bb in range(4):
+            m_v(0, bb)
+        for k in range(8):
+            e_step(1, k)
+        ld_go(2)
+        for bb in range(4):
+            m_pe(1, bb)
+        for bb in range(4):
+            m_v(1, bb)
         ld_go(3)
         for k in range(8):
             later.append((w_squares, (k,)))
@@ -436,11 +435,11 @@ def tile_cossim2d_v_kernel(tc, x, w, p, q, x_rnorm, w_rnorm, sim, grad_out, out_
             u_quant(0, g)
         t_quant(0)
         new_log(3)
+        for g in range(2):
+            u_copy(1, g)
         for yy in range(4):
             x_step(0, yy)
             a_step(3, yy)
-        for g in range(2):
-            u_copy(1, g)
         for kp in range(4):
             t_step(1, kp)
         for g in range(2):
@@ -491,16 +490,15 @@ def tile_cossim2d_v_kernel(tc, x, w, p, q, x_rnorm, w_rnorm, sim, grad_out, out_
         fill(4)
         n_quant(0)
         n_scale(2)
-        for i in range(3):
-            n_copy(2, i)
         r0 = big.tile([P, NH, 128], F32, name="r0", offset=O_R0, align_bytes=64)
         r2 = big.tile([P, NH, 128], F32, name="r2", offset=O_R2, align_bytes=64)
+        nc.gpsimd.memset(r0[:], 0.0)
+        nc.gpsimd.memset(r2[:], 0.0)
+        for i in range(3):
+            n_copy(2, i)
         for yy in range(4):
             x_step(3, yy)
             fill(5)
-            if yy == 1:
-                nc.gpsimd.memset(r0[:], 0.0)
-                nc.gpsimd.memset(r2[:], 0.0)
             if yy == 0:
                 n_quant(1)
                 n_scale(3)
@@ -619,7 +617,7 @@ def tile_cossim2d_v_kernel(tc, x, w, p, q, x_rnorm, w_rnorm, sim, grad_out, out_
             ps = bank("ts" if n % 2 == 0 else "tv")
             for t in range(4):
                 nc.tensor.transpose(ps[:, t * 128 : (t + 1) * 128], f1[:, 4 * g + t, kd * 128 : (kd + 1) * 128], ident[:])
-            ot = big.tile([P, 512], F32, name="ot%d_%d" % (g, kd), offset=O_OT[n % 4], align_bytes=64)
+            ot = big.tile([P, 512], F32, name="ot%d_%d" % (g, kd), offset=O_OT[n % 8], align_bytes=64)
             if g == 1 and n % 2 == 1:
                 nc.vector.tensor_copy(out=ot[:].rearrange("p (u t) -> p u t", t=4), in_=ps[:].rearrange("p (t u) -> p u t", t=4))
             else:

from contextlib import ExitStack

import concourse.mybir as mybir
from concourse.masks import make_identity

F32 = mybir.dt.float32
BF16 = mybir.dt.bfloat16
I32 = mybir.dt.int32
U32 = mybir.dt.uint32
U8 = mybir.dt.uint8
E4 = mybir.dt.float8_e4m3fn_x4
E5 = mybir.dt.float8_e5m2_x4
ALU = mybir.AluOpType
ACT = mybir.ActivationFunctionType
AX = mybir.AxisListType

P = 128
NB = 8
NH = 18
NY = 16
U = 1024
D = 1152
T = 2048
FLOPS = 2 * 2 * T * D * U

DX_WINDOWS = ((0, 0), (384, 0), (640, 128))
DW_WINDOWS = ((0, 0, 512, 0), (512, 0, 512, 512))

O_DTC = 0
O_DTS = 16384
O_XC = 20480
O_HA = 34304
O_WT = 61952
O_WNC = 80384
O_WNS = 89600
O_SIM = (91904, 108288)
O_LG = (124672, 141056)
O_GO = (157440, 165632)
O_UF = (173824, 177920, 221696, 225792)
O_PL = (182016, 190208)
O_UC = (198400, 202496)
O_US = (206592, 207616)
O_TF = 208640
O_JV = 216832
O_JS = 218368
O_XNC = 157440
O_XNS = 175872
O_WSB = 0
O_WN = 34304
O_JW = 194304
O_F1 = 91904
O_R0 = 182016
O_R2 = 191232
O_OT = (128768, 130816, 132864, 134912, 136960, 139008, 141056, 143104)
O_JC = 155392
O_JW2 = 219392
O_XI = (108288, 117504)
O_XS = (126720, 135936)

U_ON_SCALAR = ((3, 0), (3, 1))
N_ON_SCALAR = (0, 1)


def tile_cossim2d_v_kernel(tc, x, w, p, q, x_rnorm, w_rnorm, sim, grad_out, out_0, out_1):
    nc = tc.nc

    with ExitStack() as ctx:
        keep = ctx.enter_context(tc.tile_pool(name="keep", bufs=1))
        big = ctx.enter_context(tc.tile_pool(name="big", bufs=1))
        psum = ctx.enter_context(tc.psum_pool(name="psum", bufs=2))
        ctx.enter_context(tc.manual_schedule())

        def bank(kind):
            ps = psum.tile([P, 512], F32, name="ps_" + kind, tag=kind, bufs=4 if kind == "mm" else 2)
            return ps

        ident = keep.tile([P, P], F32, name="ident")
        make_identity(nc, ident[:])
        perm = keep.tile([P, P], F32, name="perm")
        nc.gpsimd.memset(perm[:], 0.0)
        nc.gpsimd.affine_select(
            out=perm[:], in_=perm[:], compare_op=ALU.not_equal, fill=1.0, base=0,
            pattern=[[-16, 2], [-32, 4], [-1, 16]], channel_multiplier=1,
        )
        eps_c = keep.tile([P, 1], F32, name="eps_c")
        nc.vector.memset(eps_c[:], 1e-6)
        p_c = keep.tile([P, 8], BF16, name="p_c")
        rw_c = keep.tile([P, 8], F32, name="rw_c")
        q_c = keep.tile([P, 1], BF16, name="q_c")
        rx_c = keep.tile([P, NY], F32, name="rx_c")
        rx_t = keep.tile([P, 14, 2], F32, name="rx_t")
        nc.sync.dma_start(out=p_c[:].rearrange("p (g t) -> p g t", g=2), in_=p.rearrange("(g p t) -> p g t", g=2, t=4))
        nc.sync.dma_start(out=rw_c[:].rearrange("p (g t) -> p g t", g=2), in_=w_rnorm.rearrange("(g p t) -> p g t", g=2, t=4))
        nc.sync.dma_start(out=q_c[:], in_=q.partition_broadcast(P))

        wn_codes = big.tile([P, 2, D], U32, name="wn_codes", offset=O_WNC, align_bytes=64)
        wn_scales = big.tile([P, 2, D], U8, name="wn_scales", offset=O_WNS, align_bytes=64)
        xn_codes = big.tile([P, 4, D], U32, name="xn_codes", offset=O_XNC, align_bytes=64)
        xn_scales = big.tile([P, 4, D], U8, name="xn_scales", offset=O_XNS, align_bytes=64)
        dt_codes = big.tile([P, 4, U], U32, name="dt_codes", offset=O_DTC, align_bytes=64)
        dt_scales = big.tile([P, 4, U], U8, name="dt_scales", offset=O_DTS, align_bytes=64)
        xc = big.tile([P, NH, 384], BF16, name="xc", offset=O_XC, align_bytes=64)
        ha = big.tile([P, NH, 384], F32, name="ha", offset=O_HA, align_bytes=64)
        wt = big.tile([P, 2, D, 4], BF16, name="wt", offset=O_WT, align_bytes=64)
        junk_v = big.tile([P, 384], F32, name="junk_v", offset=O_JV, align_bytes=64)
        junk_s = big.tile([P, 384], BF16, name="junk_s", offset=O_JS, align_bytes=64)
        sw_c = keep.tile([P, 8], F32, name="sw_c")
        rs_c = keep.tile([P, NH], F32, name="rs_c")
        cx_p = keep.tile([P, NY, 3], F32, name="cx_p")
        cw_p = keep.tile([P, 8, 3], F32, name="cw_p")
        e_c = keep.tile([P, 8], F32, name="e_c")
        em1_c = keep.tile([P, 8], F32, name="em1_c")
        lne_c = keep.tile([P, 8], F32, name="lne_c")
        qq_c = keep.tile([P, 1], F32, name="qq_c")

        sims = {}
        logs = {}
        gos = {}
        plains = {}
        ucodes = {}
        tfs = {}
        xts = {}

        def chunk_off(yy):
            return (yy % 2) * 256 + (yy // 2) * 128

        w_sb = big.tile([P, 9, U], BF16, name="w_sb", offset=O_WSB, align_bytes=64)

        def ld_w():
            for k0 in range(0, 9, 3):
                nc.sync.dma_start(out=w_sb[:, k0 : k0 + 3, :], in_=w[0, 128 * k0 : 128 * (k0 + 3), :].rearrange("(k p) u -> p k u", p=P))

        def ld_sim(c):
            s_sb = big.tile([P, 4, U], F32, name="s_sb%d" % c, offset=O_SIM[c % 2], align_bytes=64)
            sims[c] = s_sb
            hh, bq = c // 2, c % 2
            for bb in range(4):
                nc.sync.dma_start(out=s_sb[:, bb, :], in_=sim[4 * bq + bb, 8 * hh : 8 * hh + 8].rearrange("y z u -> (y z) u"))

        def ld_go(c):
            go = big.tile([P, 4, U], BF16, name="go%d" % c, offset=O_GO[c % 2], align_bytes=64)
            gos[c] = go
            hh, bq = c // 2, c % 2
            for b2 in range(2):
                nc.sync.dma_start(
                    out=go[:, 2 * b2 : 2 * b2 + 2, :],
                    in_=grad_out[4 * bq + 2 * b2 : 4 * bq + 2 * b2 + 2, 8 * hh : 8 * hh + 8].rearrange("b y z u -> (y z) b u"),
                )

        def ld_xc(js):
            xc4 = xc[:].rearrange("p h (j c) -> p h j c", j=3)
            for j in js:
                for b in range(NB):
                    nc.sync.dma_start(out=xc4[b:P:8, :, j, :], in_=x[b, :, j : j + 16, :].rearrange("h v c -> v h c"))

        def ld_rxc():
            with nc.allow_non_contiguous_dma(reason="2048 single floats, once"):
                for b in range(NB):
                    nc.sync.dma_start(out=rx_c[b:P:8, :], in_=x_rnorm[b].rearrange("y z -> z y"))

        def ld_rxt():
            for yh in range(2):
                for zw in range(8):
                    nc.sync.dma_start(
                        out=rx_t[64 * yh + zw : 64 * yh + 64 : 8, :, :], in_=x_rnorm[:, 2 * yh : 2 * yh + 14, 2 * zw : 2 * zw + 2]
                    )

        def ld_xw():
            xw = big.tile([P, 16, 512], BF16, name="xw", offset=O_SIM[0], align_bytes=64)
            xts[0] = xw
            xw4 = xw[:].rearrange("p r (a m) -> p r a m", a=2)
            for yh in range(2):
                for a in range(2):
                    for zw in range(8):
                        v0 = 2 * a + 2 * zw
                        nc.sync.dma_start(
                            out=xw4[64 * yh + zw : 64 * yh + 64 : 8, :, a, :],
                            in_=x[:, 2 * yh : 2 * yh + 16, v0 : v0 + 2, :].rearrange("b r e c -> b r (e c)"),
                        )

        def small_consts():
            nc.scalar.activation(out=e_c[:], in_=p_c[:], func=ACT.Square, scale=0.2)
            nc.vector.tensor_scalar_add(out=em1_c[:], in0=e_c[:], scalar1=-1.0)
            nc.scalar.activation(out=lne_c[:], in_=e_c[:], func=ACT.Ln)
            nc.scalar.activation(out=qq_c[:], in_=q_c[:], func=ACT.Square, scale=1.0 / 0.3)

        def w_turn(k0):
            ww = w_sb[:].rearrange("p k u -> p (k u)").bitcast(F32)
            wtw = wt[:].rearrange("p g d t -> p (g d t)").bitcast(F32).rearrange("p (g d h) -> p g d h", g=2, h=2)
            for g in range(2):
                for nk in (min(2, 9 - k0),):
                    ps = bank("ts")
                    for h in range(2):
                        for kk in range(nk):
                            c0 = (k0 + kk) * 512 + 256 * g
                            nc.tensor.transpose(ps[:, h * 256 + kk * 128 : h * 256 + (kk + 1) * 128], ww[:, c0 + h : c0 + 256 : 2], ident[:])
                    nc.scalar.copy(
                        out=wtw[:, g, k0 * 128 : (k0 + nk) * 128, :],
                        in_=ps[:].rearrange("p (h c) -> p c h", h=2)[:, 0 : nk * 128, :],
                    )

        wn = big.tile([P, 2, D, 4], BF16, name="wn", offset=O_WN, align_bytes=64)

        def w_scale(k0):
            d0, d1 = 128 * k0, min(128 * (k0 + 2), D)
            for g in range(2):
                nc.vector.tensor_tensor(
                    out=wn[:, g, d0:d1], in0=wt[:, g, d0:d1],
                    in1=rw_c[:, 4 * g : 4 * g + 4].unsqueeze(1).to_broadcast([P, d1 - d0, 4]), op=ALU.mult,
                )

        def w_quant():
            wnf = wn[:].rearrange("p g d t -> p g (d t)")
            for g in range(2):
                for d0, d1 in ((0, 1024), (1024, D)):
                    nc.vector.quantize_mx(
                        out=wn_codes[:, g, d0:d1].bitcast(E4), scales=wn_scales[:, g, d0:d1], in_=wnf[:, g, 4 * d0 : 4 * d1]
                    )

        junk_w = big.tile([P, D], BF16, name="junk_w", offset=O_JW2, align_bytes=64)

        def w_squares(k):
            nc.scalar.activation(out=junk_w[:], in_=wt[:, k // 4, :, k % 4], func=ACT.Square, accum_out=sw_c[:, k : k + 1])

        def x_squares(h):
            nc.scalar.activation(out=junk_s[:], in_=xc[:, h, :], func=ACT.Square, accum_out=rs_c[:, h : h + 1])

        def new_log(c):
            logs[c] = big.tile([P, 8, 512], F32, name="lg%d" % c, offset=O_LG[c % 2], align_bytes=64)

        def v_abs(c, yy):
            v = sims[c][:, yy, :].bitcast(I32)
            nc.vector.tensor_scalar(out=v, in0=v, scalar1=0x7FFFFFFF, scalar2=None, op0=ALU.bitwise_and)

        def a_step(c, yy):
            s_sb = sims[c]
            lg = logs[c]
            off = 128 * yy
            for g in range(2):
                ps = bank("ts")
                for t in range(4):
                    nc.tensor.transpose(ps[:, t * 128 : (t + 1) * 128], s_sb[:, yy, 512 * g + t : 512 * (g + 1) : 4], perm[:])
                nc.scalar.activation(
                    out=lg[:, 4 * g : 4 * g + 4, off : off + 128],
                    in_=ps[:].rearrange("p (t c) -> p t c", t=4),
                    func=ACT.Ln,
                    bias=eps_c[:, 0:1],
                )

        def e_step(c, k):
            lg = logs[c]
            nc.scalar.activation(out=lg[:, k, :], in_=lg[:, k, :], func=ACT.Exp, bias=lne_c[:, k : k + 1], scale=em1_c[:, k : k + 1])

        def new_plain(hh):
            plains[hh] = big.tile([P, 8, 1024], BF16, name="pl%d" % hh, offset=O_PL[0], align_bytes=64)

        gts = {}

        def m_pe(c, yy):
            gw = gos[c][:].rearrange("p y u -> p (y u)").bitcast(F32)
            ps = bank("mm" if c < 2 and yy >= 2 else "tv")
            gts[(c, yy)] = ps
            for gh in range(4):
                c0 = yy * 512 + 256 * (gh // 2)
                nc.tensor.transpose(ps[:, gh * 128 : (gh + 1) * 128], gw[:, c0 + gh % 2 : c0 + 256 : 2], perm[:])

        def m_v(c, yy):
            b = 4 * (c % 2) + yy
            pl6 = plains[c // 2][:].rearrange("p (k e) (r b z) -> p k e r b z", e=2, r=8, b=NB)
            lg5 = logs[c][:, :, 128 * yy : 128 * yy + 128].rearrange("p (k e) (r z) -> p k e r z", e=2, r=8)
            ps5 = gts[(c, yy)][:].bitcast(BF16).rearrange("p (k r z e) -> p k e r z", k=4, r=8, e=2)
            for e in range(2):
                nc.vector.tensor_tensor(out=pl6[:, :, e, :, b, :], in0=lg5[:, :, e], in1=ps5[:, :, e], op=ALU.mult)

        def u_copy(c, g):
            if g == 0:
                uc = big.tile([P, 2, 512], U32, name="uc%d" % c, offset=O_UC[c % 2], align_bytes=64)
                us = big.tile([P, 2, 512], U8, name="us%d" % c, offset=O_US[c % 2], align_bytes=64)
                ucodes[c] = [uc, us, None, None]
            uf = big.tile([P, 512, 4], BF16, name="uf%d_%d" % (c, g), offset=O_UF[2 * (c % 2) + g], align_bytes=64)
            ucodes[c][2 + g] = uf
            for yy in range(4):
                s0 = (yy % 2) * 512 + (2 * (c % 2) + yy // 2) * 128
                src = plains[c // 2][:, 4 * g : 4 * g + 4, s0 : s0 + 128].rearrange("p t (b z) -> p z b t", b=NB)
                dst = uf[:, chunk_off(yy) : chunk_off(yy) + 128, :].rearrange("p (z b) t -> p z b t", b=NB)
                if c % 2 == 1:
                    nc.gpsimd.tensor_scalar(out=dst, in0=src, scalar1=1.0, scalar2=0.0, op0=ALU.mult, op1=ALU.add)
                else:
                    nc.vector.tensor_copy(out=dst, in_=src)

        def u_quant(c, g):
            uc, us = ucodes[c][0], ucodes[c][1]
            uf = ucodes[c][2 + g]
            nc.vector.quantize_mx(out=uc[:, g, :].bitcast(E5), scales=us[:, g, :], in_=uf[:].rearrange("p c t -> p (c t)"))

        def t_step(c, kp):
            if kp == 0:
                tfs[c] = big.tile([P, U, 4], BF16, name="tf%d" % c, offset=O_TF, align_bytes=64)
            plw = plains[c // 2][:].rearrange("p k c -> p (k c)").bitcast(F32)
            tfw = tfs[c][:].rearrange("p u t -> p (u t)").bitcast(F32).rearrange("p (u l) -> p u l", l=2)
            ps = bank("ts")
            for l in range(2):
                for kk in range(2):
                    c0 = (2 * kp + kk) * 512 + l * 256 + (c % 2) * 128
                    nc.tensor.transpose(ps[:, l * 256 + kk * 128 : l * 256 + (kk + 1) * 128], plw[:, c0 : c0 + 128], ident[:])
            nc.scalar.copy(out=tfw[:, kp * 256 : (kp + 1) * 256, :], in_=ps[:].rearrange("p (l c) -> p c l", l=2))

        def t_quant(c):
            nc.vector.quantize_mx(out=dt_codes[:, c, :].bitcast(E5), scales=dt_scales[:, c, :], in_=tfs[c][:].rearrange("p u t -> p (u t)"))

        touched = set()

        def x_step(c, yy):
            uc, us = ucodes[c][0], ucodes[c][1]
            y = 4 * c + yy
            co = chunk_off(yy)
            for i in (2, 0, 1):
                ws, uo = DX_WINDOWS[i]
                ps = bank("mm")
                for g in range(2):
                    nc.tensor.matmul_mx(
                        out=ps[:],
                        lhsT=uc[:, g, co : co + 128].bitcast(E5),
                        lhsT_scale=us[:, g, co : co + 128],
                        rhs=wn_codes[:, g, ws : ws + 512].bitcast(E4),
                        rhs_scale=wn_scales[:, g, ws : ws + 512],
                        start=(g == 0),
                        stop=(g == 1),
                    )
                h = y + i
                if h not in touched:
                    touched.add(h)
                    nc.scalar.activation(out=ha[:, h, :], in_=ps[:, uo : uo + 384], func=ACT.Copy, scale=rx_c[:, y : y + 1])
                else:
                    nc.vector.scalar_tensor_tensor(
                        out=ha[:, h, :], in0=ps[:, uo : uo + 384], scalar=rx_c[:, y : y + 1], in1=ha[:, h, :], op0=ALU.mult, op1=ALU.add
                    )
                nc.vector.scalar_tensor_tensor(
                    out=junk_v[:], in0=ps[:, uo : uo + 384], scalar=1.0, in1=xc[:, h, :],
                    op0=ALU.mult, op1=ALU.mult, accum_out=cx_p[:, y, i : i + 1],
                )

        def n_scale(c):
            xw = xts[0]
            xs = big.tile([P, 4, 3, 384], BF16, name="xs%d" % c, offset=O_XS[c % 2], align_bytes=64)
            xts[("s", c)] = xs
            for l in range(2):
                for e in range(2):
                    r0 = 4 * c + l
                    nc.vector.tensor_scalar_mul(
                        out=xs[:, 2 * l + e, :, :], in0=xw[:, r0 : r0 + 3, e * 128 : e * 128 + 384], scalar1=rx_t[:, r0, e : e + 1]
                    )

        def n_copy(c, i):
            if i == 0:
                xts[("i", c)] = big.tile([P, D, 4], BF16, name="xi%d" % c, offset=O_XI[c % 2], align_bytes=64)
            xi = xts[("i", c)]
            src = xts[("s", c)][:, :, i, :].rearrange("p t m -> p m t")
            if c in N_ON_SCALAR:
                nc.scalar.copy(out=xi[:, 384 * i : 384 * (i + 1), :], in_=src)
            else:
                nc.gpsimd.tensor_scalar(out=xi[:, 384 * i : 384 * (i + 1), :], in0=src, scalar1=1.0, scalar2=0.0, op0=ALU.mult, op1=ALU.add)

        def n_quant(c):
            xif = xts[("i", c)][:].rearrange("p d t -> p (d t)")
            for d0, d1 in ((0, 1024), (1024, D)):
                nc.vector.quantize_mx(out=xn_codes[:, c, d0:d1].bitcast(E4), scales=xn_scales[:, c, d0:d1], in_=xif[:, 4 * d0 : 4 * d1])

        later = []

        def fill(n):
            for r in range(min(n, len(later))):
                f, a = later.pop(0)
                f(*a)

        ld_w()
        ld_sim(0)
        ld_sim(1)
        ld_go(0)
        ld_go(1)
        ld_rxc()
        small_consts()
        for k0 in range(0, 9, 2):
            w_turn(k0)
        new_log(0)
        w_scale(0)
        w_scale(2)
        for bb in range(4):
            v_abs(0, bb)
            a_step(0, bb)
            if bb < 3:
                w_scale(4 + 2 * bb)
        for bb in range(4):
            v_abs(1, bb)
        new_log(1)
        for bb in range(4):
            a_step(1, bb)
        for k in range(8):
            e_step(0, k)
        for bb in range(4):
            m_pe(0, bb)
        ld_sim(2)
        ld_sim(3)
        ld_xc((0, 1, 2))
        w_quant()
        for bb in range(4):
            v_abs(2, bb)
        new_plain(0)
        for bb in range(4):
            m_v(0, bb)
        for k in range(8):
            e_step(1, k)
        ld_go(2)
        for bb in range(4):
            m_pe(1, bb)
        for bb in range(4):
            m_v(1, bb)
        ld_go(3)
        for k in range(8):
            later.append((w_squares, (k,)))
        for h in range(NH):
            later.append((x_squares, (h,)))
        new_log(2)
        for bb in range(4):
            a_step(2, bb)
        ld_xw()
        ld_rxt()
        for g in range(2):
            u_copy(0, g)
        for kp in range(4):
            t_step(0, kp)
        for bb in range(4):
            v_abs(3, bb)
        for g in range(2):
            u_quant(0, g)
        t_quant(0)
        new_log(3)
        for g in range(2):
            u_copy(1, g)
        for yy in range(4):
            x_step(0, yy)
            a_step(3, yy)
        for kp in range(4):
            t_step(1, kp)
        for g in range(2):
            u_quant(1, g)
        t_quant(1)
        m_pe(2, 0)
        m_pe(2, 1)
        for yy in range(4):
            x_step(1, yy)
            for k in range(4 * (yy % 2), 4 * (yy % 2) + 4):
                e_step(2 + yy // 2, k)
        fill(6)
        new_plain(1)
        for c in (2, 3):
            if c == 3:
                m_pe(3, 0)
                m_pe(3, 1)
            m_v(c, 0)
            m_pe(c, 2)
            m_v(c, 1)
            m_pe(c, 3)
            m_v(c, 2)
            m_v(c, 3)
        for g in range(2):
            u_copy(2, g)
        for kp in range(4):
            t_step(2, kp)
        n_scale(0)
        for g in range(2):
            u_quant(2, g)
        t_quant(2)
        n_scale(1)
        for c in range(2):
            for i in range(3):
                later.insert(3 * c + i, (n_copy, (c, i)))
        for yy in range(4):
            x_step(2, yy)
            if yy < 2:
                u_copy(3, yy)
                t_step(3, 2 * yy)
                t_step(3, 2 * yy + 1)
            else:
                fill(1)
            if yy == 2:
                for g in range(2):
                    u_quant(3, g)
                t_quant(3)
        fill(4)
        n_quant(0)
        n_scale(2)
        r0 = big.tile([P, NH, 128], F32, name="r0", offset=O_R0, align_bytes=64)
        r2 = big.tile([P, NH, 128], F32, name="r2", offset=O_R2, align_bytes=64)
        nc.gpsimd.memset(r0[:], 0.0)
        nc.gpsimd.memset(r2[:], 0.0)
        for i in range(3):
            n_copy(2, i)
        for yy in range(4):
            x_step(3, yy)
            fill(5)
            if yy == 0:
                n_quant(1)
                n_scale(3)
                for i in range(3):
                    n_copy(3, i)
        fill(len(later))

        sx = keep.tile([P, NY], F32, name="sx")
        fx = keep.tile([P, NY], F32, name="fx")
        cx = keep.tile([P, NY], F32, name="cx")
        ns = keep.tile([P, NH], F32, name="ns")
        fw = keep.tile([P, 8], F32, name="fw")
        rsw = keep.tile([P, 8], F32, name="rsw")
        cw = keep.tile([P, 8], F32, name="cw")
        f1 = big.tile([P, 8, D], F32, name="f1", offset=O_F1, align_bytes=64)
        junk_c = big.tile([P, 512], F32, name="junk_c", offset=O_JC, align_bytes=64)
        ha4 = ha[:].rearrange("p h (j c) -> p h j c", j=3)
        flat1 = out_1.rearrange("o d u -> (o d u)")
        park0 = flat1[0 : P * NH * 128].rearrange("(p h c) -> p h c", p=P, c=128)
        park2 = flat1[P * NH * 128 : 2 * P * NH * 128].rearrange("(p h c) -> p h c", p=P, c=128)

        def dw_mm(k):
            for wi in range(2):
                ws = DW_WINDOWS[wi][0]
                ps = bank("mm")
                for c in range(4):
                    nc.tensor.matmul_mx(
                        out=ps[:],
                        lhsT=dt_codes[:, c, k * 128 : (k + 1) * 128].bitcast(E5),
                        lhsT_scale=dt_scales[:, c, k * 128 : (k + 1) * 128],
                        rhs=xn_codes[:, c, ws : ws + 512].bitcast(E4),
                        rhs_scale=xn_scales[:, c, ws : ws + 512],
                        start=(c == 0),
                        stop=(c == 3),
                    )
                ws, uo, n, d0 = DW_WINDOWS[wi]
                nc.vector.scalar_tensor_tensor(
                    out=junk_c[:, 0:n], in0=ps[:, uo : uo + n], scalar=1.0, in1=wt[:, k // 4, d0 : d0 + n, k % 4],
                    op0=ALU.mult, op1=ALU.mult, accum_out=cw_p[:, k, wi : wi + 1],
                )
                nc.scalar.activation(out=f1[:, k, d0 : d0 + n], in_=ps[:, uo : uo + n], func=ACT.Copy, scale=rw_c[:, k : k + 1])

        def dw_last(g):
            ps = bank("mm")
            for c in range(4):
                nc.tensor.matmul_mx(
                    out=ps[:],
                    lhsT=xn_codes[:, c, 1024:D].bitcast(E4),
                    lhsT_scale=xn_scales[:, c, 1024:D],
                    rhs=dt_codes[:, c, 512 * g : 512 * (g + 1)].bitcast(E5),
                    rhs_scale=dt_scales[:, c, 512 * g : 512 * (g + 1)],
                    start=(c == 0),
                    stop=(c == 3),
                )
            d8 = big.tile([P, 512], F32, name="d8_%d" % g, offset=O_OT[g], align_bytes=64)
            nc.scalar.copy(out=d8[:], in_=ps[:])
            ps2 = bank("ts")
            for t in range(4):
                nc.tensor.transpose(ps2[:, t * 128 : (t + 1) * 128], d8[:, t * 128 : (t + 1) * 128], ident[:])
            for t in range(4):
                k = 4 * g + t
                nc.vector.scalar_tensor_tensor(
                    out=junk_c[:, 0:128], in0=ps2[:, t * 128 : (t + 1) * 128], scalar=1.0, in1=wt[:, g, 1024:D, t],
                    op0=ALU.mult, op1=ALU.mult, accum_out=cw_p[:, k, 2:3],
                )
                nc.scalar.activation(out=f1[:, k, 1024:D], in_=ps2[:, t * 128 : (t + 1) * 128], func=ACT.Copy, scale=rw_c[:, k : k + 1])

        def x_factors():
            nc.vector.tensor_tensor(out=sx[:], in0=rs_c[:, 0:16], in1=rs_c[:, 1:17], op=ALU.add)
            nc.vector.tensor_tensor(out=sx[:], in0=sx[:], in1=rs_c[:, 2:18], op=ALU.add)
            nc.vector.reciprocal(out=sx[:], in_=sx[:])
            nc.vector.tensor_scalar(out=fx[:], in0=rx_c[:], scalar1=qq_c[:, 0:1], scalar2=-1.0, op0=ALU.mult, op1=ALU.add)
            nc.vector.tensor_tensor(out=fx[:], in0=fx[:], in1=rx_c[:], op=ALU.mult)
            nc.vector.tensor_tensor(out=fx[:], in0=fx[:], in1=sx[:], op=ALU.mult)
            nc.vector.tensor_reduce(out=cx[:], in_=cx_p[:], axis=AX.X, op=ALU.add)
            nc.vector.tensor_tensor(out=cx[:], in0=cx[:], in1=fx[:], op=ALU.mult)
            nc.vector.memset(ns[:], 0.0)
            for i in range(3):
                nc.vector.tensor_tensor(out=ns[:, i : i + 16], in0=ns[:, i : i + 16], in1=cx[:], op=ALU.add)

        def w_factors():
            nc.vector.reciprocal(out=rsw[:], in_=sw_c[:])
            nc.vector.tensor_scalar(out=fw[:], in0=rw_c[:], scalar1=qq_c[:, 0:1], scalar2=-1.0, op0=ALU.mult, op1=ALU.add)
            nc.vector.tensor_tensor(out=fw[:], in0=fw[:], in1=rw_c[:], op=ALU.mult)
            nc.vector.tensor_tensor(out=fw[:], in0=fw[:], in1=rsw[:], op=ALU.mult)

        def x_norm_term(h):
            nc.vector.scalar_tensor_tensor(
                out=ha[:, h, :], in0=xc[:, h, :], scalar=ns[:, h : h + 1], in1=ha[:, h, :], op0=ALU.mult, op1=ALU.add
            )

        def park():
            nc.sync.dma_start(out=park0, in_=ha4[:, :, 0, :])
            nc.sync.dma_start(out=park2, in_=ha4[:, :, 2, :])
            nc.sync.dma_start(out=out_0[:, :, 0, :], in_=ha4[0:8, :, 0, :])
            nc.sync.dma_start(out=out_0[:, :, 17, :], in_=ha4[120:128, :, 2, :])
            nc.sync.dma_start(out=r0[0:120], in_=park0[8:128])
            nc.sync.dma_start(out=r2[8:128], in_=park2[0:120])

        def x_finish():
            nc.vector.tensor_tensor(out=r0[:], in0=r0[:], in1=ha4[:, :, 1, :], op=ALU.add)
            nc.vector.tensor_tensor(out=r0[:], in0=r0[:], in1=r2[:], op=ALU.add)
            for b in range(NB):
                nc.sync.dma_start(out=out_0[b, :, 1:17, :].rearrange("h v c -> v h c"), in_=r0[b:P:8])

        def w_coef(k):
            nc.vector.tensor_reduce(out=cw[:, k : k + 1], in_=cw_p[:, k, :], axis=AX.X, op=ALU.add)
            nc.vector.tensor_tensor(out=cw[:, k : k + 1], in0=cw[:, k : k + 1], in1=fw[:, k : k + 1], op=ALU.mult)

        def w_final(k):
            nc.vector.scalar_tensor_tensor(
                out=f1[:, k, :], in0=wt[:, k // 4, :, k % 4], scalar=cw[:, k : k + 1], in1=f1[:, k, :], op0=ALU.mult, op1=ALU.add
            )

        def w_store(g, kd, n):
            ps = bank("ts" if n % 2 == 0 else "tv")
            for t in range(4):
                nc.tensor.transpose(ps[:, t * 128 : (t + 1) * 128], f1[:, 4 * g + t, kd * 128 : (kd + 1) * 128], ident[:])
            ot = big.tile([P, 512], F32, name="ot%d_%d" % (g, kd), offset=O_OT[n % 8], align_bytes=64)
            if g == 1 and n % 2 == 1:
                nc.vector.tensor_copy(out=ot[:].rearrange("p (u t) -> p u t", t=4), in_=ps[:].rearrange("p (t u) -> p u t", t=4))
            else:
                nc.scalar.copy(out=ot[:].rearrange("p (u t) -> p u t", t=4), in_=ps[:].rearrange("p (t u) -> p u t", t=4))
            nc.sync.dma_start(out=out_1[0, kd * 128 : (kd + 1) * 128, 512 * g : 512 * (g + 1)], in_=ot[:])

        x_factors()
        for h in range(NH):
            x_norm_term(h)
        park()
        n_quant(2)
        n_quant(3)
        w_factors()
        dw_last(0)
        dw_last(1)
        for k in range(4):
            dw_mm(k)
            w_coef(k)
            w_final(k)
            if k == 1:
                x_finish()
        for k in range(4, 8):
            dw_mm(k)
            w_coef(k)
            w_final(k)
            for n in range(3 * (k - 4), min(3 * (k - 4) + 3, 9)):
                w_store(0, 8 - n, n)
        for n in range(9):
            w_store(1, 8 - n, n + 1)
